import numpy as np
import ml_dtypes

BF16 = ml_dtypes.bfloat16


def bf(x):
    return np.asarray(x, np.float32).astype(BF16)


def f32(x):
    return np.asarray(x, np.float32)


def f64(x):
    return np.asarray(x).astype(np.float64)


def striped(idx):
    return np.tile(idx.reshape(-1, 16).T, (8, 1))


DIM, D2, D3, S, R, NH, HD, N, HALF, RUNS = 512, 1024, 1536, 2048, 4, 8, 64, 8192, 1024, 8
SCALE = 1.0 / np.sqrt(HD)


def setup_inputs():
    x = f32(np.random.standard_normal((DIM, S)))
    wqkv = bf(np.random.standard_normal((DIM, D3)) / np.sqrt(DIM))
    bq = f32(0.1 * np.random.standard_normal((DIM, 1)))
    bv = f32(0.1 * np.random.standard_normal((DIM, 1)))
    wout = bf(np.random.standard_normal((DIM, DIM)) / np.sqrt(DIM))
    bout = f32(0.1 * np.random.standard_normal((DIM, 1)))
    idx = np.concatenate([np.random.permutation(S)[:HALF] for _ in range(RUNS)])
    return {"x": x, "wqkv": wqkv, "bq": bq, "bv": bv, "wout": wout, "bout": bout, "offs": striped(idx)}


def reference(x, wqkv, bq, bv, wout, bout, offs):
    idx = offs[:16].T.reshape(-1)
    xx = f64(x)
    w = f64(wqkv)
    q = w[:, :DIM].T @ xx + f64(bq)
    key = w[:, DIM:D2].T @ xx
    val = w[:, D2:].T @ xx + f64(bv)
    kv = np.concatenate([key, val], axis=0)
    kvg = kv[:, idx].reshape(D2, R, S)
    prod = kvg[:DIM] * q[:, None, :]
    sc = SCALE * prod.reshape(NH, HD, R, S).sum(axis=1)
    e = np.exp(sc)
    p = np.repeat(e / e.sum(axis=1, keepdims=True), HD, axis=0)
    att = (kvg[DIM:] * p).sum(axis=1)
    return f64(wout).T @ att + f64(bout)

@@ -1,0 +1,208 @@
+import concourse.masks as masks
+import concourse.mybir as mybir
+
+F32, BF16, U16 = mybir.dt.float32, mybir.dt.bfloat16, mybir.dt.uint16
+ALU = mybir.AluOpType
+ACT = mybir.ActivationFunctionType
+AXIS = mybir.AxisListType
+
+P = 128
+DIM = 512
+TOKENS = 2048
+ROUTES = 4
+HEAD_DIM = 64
+SCALE = 0.125
+BLOCKS = DIM // P
+BLOCK_HEADS = P // HEAD_DIM
+BANK = 512
+CHUNKS = TOKENS // BANK
+GROUPS = TOKENS // P
+CHUNK_GROUPS = BANK // P
+CHUNK_COLS = CHUNK_GROUPS * ROUTES * BLOCK_HEADS
+PARTS = 3
+ROWS = PARTS * CHUNK_COLS
+LIST_COLS = 16
+
+FLOPS = 2 * DIM * 3 * DIM * TOKENS + 2 * DIM * DIM * TOKENS + 4 * DIM * ROUTES * TOKENS
+
+
+def tile_cantorattention_b_kernel(tc, x, wqkv, bq, bv, wout, bout, offs, out):
+    nc = tc.nc
+    with (
+        tc.tile_pool(name="held", bufs=1) as held,
+        tc.tile_pool(name="tables", bufs=2) as tables,
+        tc.tile_pool(name="soft", bufs=2) as soft,
+        tc.tile_pool(name="ring", bufs=3) as ring,
+        tc.psum_pool(name="psum", bufs=2) as psum,
+    ):
+        offsets = held.tile([P, ROUTES * TOKENS // LIST_COLS], U16, name="offsets")
+        nc.sync.dma_start(offsets[:], offs)
+
+        def load_weights(name, columns):
+            w = held.tile([P, BLOCKS, DIM], BF16, name=name)
+            nc.scalar.dma_start(w[:], columns.rearrange("(kb p) c -> p kb c", p=P))
+            return w
+
+        def load_bias(name, vector):
+            bias = held.tile([P, BLOCKS], F32, name=name)
+            with nc.allow_non_contiguous_dma(reason="one bias element to a partition"):
+                nc.scalar.dma_start(bias[:], vector.rearrange("(b p) o -> p (b o)", p=P))
+            return bias
+
+        w_key = load_weights("w_key", wqkv[:, DIM : 2 * DIM])
+        w_q = load_weights("w_q", wqkv[:, 0:DIM])
+        bias_q = load_bias("bias_q", bq)
+        w_val = load_weights("w_val", wqkv[:, 2 * DIM : 3 * DIM])
+        bias_v = load_bias("bias_v", bv)
+        w_out = load_weights("w_out", wout)
+        bias_out = load_bias("bias_out", bout)
+
+        x_bf = [held.tile([P, BLOCKS, BANK], BF16, name=f"x_bf{xc}") for xc in range(CHUNKS)]
+        with tc.tile_pool(name="stage", bufs=1) as stage:
+            for xc in range(CHUNKS):
+                x_f32 = stage.tile([P, BLOCKS, BANK], F32, name=f"x_f32_{xc}")
+                nc.sync.dma_start(x_f32[:], x[:, xc * BANK : (xc + 1) * BANK].rearrange("(kb p) t -> p kb t", p=P))
+                nc.vector.tensor_copy(x_bf[xc][:], x_f32[:])
+
+        identity = held.tile([P, P], BF16, name="identity")
+        masks.make_identity(nc, identity[:])
+        head_of = held.tile([P, BLOCK_HEADS], BF16, name="head_of")
+        nc.vector.memset(head_of[:], 0.0)
+        for h in range(BLOCK_HEADS):
+            nc.vector.memset(head_of[h * HEAD_DIM : (h + 1) * HEAD_DIM, h : h + 1], 1.0)
+        stacked_two = held.tile([ROWS, CHUNK_COLS], BF16, name="stacked_two")
+        stacked = held.tile([ROWS, CHUNK_COLS], BF16, name="stacked")
+        spread = held.tile([ROWS, CHUNK_GROUPS, ROUTES, P], BF16, name="spread")
+        nc.vector.tensor_tensor(
+            stacked_two[:], identity[0:ROWS, 0:CHUNK_COLS], identity[0:ROWS, CHUNK_COLS : 2 * CHUNK_COLS], ALU.add
+        )
+        nc.vector.tensor_tensor(stacked[:], stacked_two[:], identity[0:ROWS, 2 * CHUNK_COLS : 3 * CHUNK_COLS], ALU.add)
+        nc.vector.tensor_copy(
+            spread[:].rearrange("k g r (h c) -> k (g r h) c", c=HEAD_DIM),
+            stacked[:].unsqueeze(2).to_broadcast([ROWS, CHUNK_COLS, HEAD_DIM]),
+        )
+
+        att = [held.tile([P, TOKENS], BF16, name=f"att{b}") for b in range(BLOCKS)]
+
+        def project(name, w, b, bias):
+            table = tables.tile([P, TOKENS], F32, name=name)
+            for xc in range(CHUNKS):
+                acc = psum.tile([P, BANK], F32, name="acc", bufs=3)
+                for kb in range(BLOCKS):
+                    nc.tensor.matmul(
+                        acc[:],
+                        lhsT=w[:, kb, b * P : (b + 1) * P],
+                        rhs=x_bf[xc][:, kb, :],
+                        start=(kb == 0),
+                        stop=(kb == BLOCKS - 1),
+                    )
+                if bias is None:
+                    nc.scalar.copy(table[:, xc * BANK : (xc + 1) * BANK], acc[:])
+                else:
+                    nc.scalar.activation(
+                        table[:, xc * BANK : (xc + 1) * BANK], acc[:], ACT.Identity, bias=bias[:, b : b + 1]
+                    )
+            return table
+
+        def over_routes(small):
+            return small[:].unsqueeze(2).to_broadcast([P, GROUPS, ROUTES, BLOCK_HEADS])
+
+        def by_chunk(columns):
+            return columns[:].rearrange("p (xc g) r h -> p xc (g r h)", xc=CHUNKS)
+
+        with tc.tile_pool(name="late", bufs=2) as late:
+            for b in range(BLOCKS):
+                key = project("key", w_key, b, None)
+                q = project("q", w_q, b, bias_q)
+                val = project("val", w_val, b, bias_v)
+
+                scores = psum.tile([P, GROUPS, ROUTES, BLOCK_HEADS], F32, name="scores")
+                for r in range(ROUTES):
+                    first_col = r * TOKENS // LIST_COLS
+                    prod = ring.tile([P, TOKENS], F32, name="prod")
+                    nc.vector.tensor_tensor(
+                        prod[:], key[:].indirect(offsets[:, first_col : first_col + TOKENS // LIST_COLS]), q[:], ALU.mult
+                    )
+                    prod_bf = ring.tile([P, TOKENS], BF16, name="prod_bf")
+                    nc.scalar.copy(prod_bf[:], prod[:])
+                    for g in range(GROUPS):
+                        nc.tensor.matmul(
+                            scores[:, g, r, :], lhsT=prod_bf[:, g * P : (g + 1) * P], rhs=head_of[:], start=True, stop=True
+                        )
+
+                top = soft.tile([P, GROUPS, BLOCK_HEADS], F32, name="top")
+                nc.vector.tensor_reduce(out=top[:], in_=scores[:].rearrange("p g r h -> p g h r"), axis=AXIS.X, op=ALU.max)
+                shifted = soft.tile([P, GROUPS, ROUTES, BLOCK_HEADS], F32, name="shifted")
+                nc.vector.tensor_tensor(shifted[:], scores[:], over_routes(top), ALU.subtract)
+                exps = soft.tile([P, GROUPS, ROUTES, BLOCK_HEADS], F32, name="exps")
+                nc.scalar.activation(exps[:], shifted[:], ACT.Exp, scale=SCALE)
+                total = soft.tile([P, GROUPS, BLOCK_HEADS], F32, name="total")
+                nc.vector.tensor_reduce(out=total[:], in_=exps[:].rearrange("p g r h -> p g h r"), axis=AXIS.X, op=ALU.add)
+                inverse = soft.tile([P, GROUPS, BLOCK_HEADS], F32, name="inverse")
+                nc.vector.reciprocal(inverse[:], total[:])
+                prob = soft.tile([P, GROUPS, ROUTES, BLOCK_HEADS], F32, name="prob")
+                nc.vector.tensor_tensor(prob[:], exps[:], over_routes(inverse), ALU.mult)
+
+                parts = soft.tile([P, CHUNKS, PARTS, CHUNK_COLS], BF16, name="parts")
+                rest = soft.tile([P, GROUPS, ROUTES, BLOCK_HEADS], F32, name="rest")
+                nc.vector.tensor_copy(parts[:, :, 0, :], by_chunk(prob))
+                nc.vector.tensor_tensor(by_chunk(rest), by_chunk(prob), parts[:, :, 0, :], ALU.subtract)
+                nc.vector.tensor_copy(parts[:, :, 1, :], by_chunk(rest))
+                nc.vector.tensor_tensor(parts[:, :, 2, :], by_chunk(rest), parts[:, :, 1, :], ALU.subtract)
+
+                rows_psum = psum.tile([ROWS, CHUNKS * P], BF16, name="rows_psum", bufs=1)
+                for xc in range(CHUNKS):
+                    nc.tensor.transpose(
+                        rows_psum[:, xc * P : (xc + 1) * P], parts[:, xc, :, :].rearrange("p k c -> p (k c)"), identity[:]
+                    )
+                p_rows = soft.tile([ROWS, CHUNKS * P], BF16, name="p_rows")
+                nc.scalar.copy(p_rows[:], rows_psum[:])
+
+                span = TOKENS if b < BLOCKS - 1 else BANK
+                for first in range(0, TOKENS, span):
+                    for r in range(ROUTES):
+                        p_block = late.tile([P, span], F32, name="p_block")
+                        for at in range(0, span, BANK):
+                            xc = (first + at) // BANK
+                            p_psum = psum.tile([P, BANK], F32, name="p_psum")
+                            for g in range(CHUNK_GROUPS):
+                                nc.tensor.matmul(
+                                    p_psum[:, g * P : (g + 1) * P],
+                                    lhsT=spread[:, g, r, :],
+                                    rhs=p_rows[:, xc * P : (xc + 1) * P],
+                                    start=True,
+                                    stop=True,
+                                )
+                            nc.scalar.copy(p_block[:, at : at + BANK], p_psum[:])
+                        first_col = (r * TOKENS + first) // LIST_COLS
+                        weighted = late.tile([P, span], F32, name="weighted")
+                        nc.vector.tensor_tensor(
+                            weighted[:],
+                            val[:].indirect(offsets[:, first_col : first_col + span // LIST_COLS]),
+                            p_block[:],
+                            ALU.mult,
+                        )
+                        if r == 0:
+                            summed = weighted[:]
+                        else:
+                            if r < ROUTES - 1:
+                                longer = late.tile([P, span], F32, name="longer")[:]
+                            else:
+                                longer = att[b][:, first : first + span]
+                            nc.vector.tensor_tensor(longer, summed, weighted[:], ALU.add)
+                            summed = longer
+
+                    if b == BLOCKS - 1:
+                        for ob in range(BLOCKS):
+                            acc = psum.tile([P, BANK], F32, name="acc", bufs=3)
+                            for kb in range(BLOCKS):
+                                nc.tensor.matmul(
+                                    acc[:],
+                                    lhsT=w_out[:, kb, ob * P : (ob + 1) * P],
+                                    rhs=att[kb][:, first : first + BANK],
+                                    start=(kb == 0),
+                                    stop=(kb == BLOCKS - 1),
+                                )
+                            result = late.tile([P, BANK], F32, name="result")
+                            nc.scalar.activation(result[:], acc[:], ACT.Identity, bias=bias_out[:, ob : ob + 1])
+                            nc.sync.dma_start(out[ob * P : (ob + 1) * P, first : first + BANK], result[:])

@@ -13,6 +13,7 @@ ROUTES = 4
 HEAD_DIM = 64
 SCALE = 0.125
 BLOCKS = DIM // P
+LAST = BLOCKS - 1
 BLOCK_HEADS = P // HEAD_DIM
 BANK = 512
 CHUNKS = TOKENS // BANK
@@ -38,9 +39,13 @@ def tile_cantorattention_b_kernel(tc, x, wqkv, bq, bv, wout, bout, offs, out):
         offsets = held.tile([P, ROUTES * TOKENS // LIST_COLS], U16, name="offsets")
         nc.sync.dma_start(offsets[:], offs)
 
-        def load_weights(name, columns):
+        def route_offsets(r, first, count):
+            column = (r * TOKENS + first) // LIST_COLS
+            return offsets[:, column : column + count // LIST_COLS]
+
+        def load_weights(queue, name, columns):
             w = held.tile([P, BLOCKS, DIM], BF16, name=name)
-            nc.scalar.dma_start(w[:], columns.rearrange("(kb p) c -> p kb c", p=P))
+            queue.dma_start(w[:], columns.rearrange("(kb p) c -> p kb c", p=P))
             return w
 
         def load_bias(name, vector):
@@ -48,21 +53,6 @@ def tile_cantorattention_b_kernel(tc, x, wqkv, bq, bv, wout, bout, offs, out):
             with nc.allow_non_contiguous_dma(reason="one bias element to a partition"):
                 nc.scalar.dma_start(bias[:], vector.rearrange("(b p) o -> p (b o)", p=P))
             return bias
-
-        w_key = load_weights("w_key", wqkv[:, DIM : 2 * DIM])
-        w_q = load_weights("w_q", wqkv[:, 0:DIM])
-        bias_q = load_bias("bias_q", bq)
-        w_val = load_weights("w_val", wqkv[:, 2 * DIM : 3 * DIM])
-        bias_v = load_bias("bias_v", bv)
-        w_out = load_weights("w_out", wout)
-        bias_out = load_bias("bias_out", bout)
-
-        x_bf = [held.tile([P, BLOCKS, BANK], BF16, name=f"x_bf{xc}") for xc in range(CHUNKS)]
-        with tc.tile_pool(name="stage", bufs=1) as stage:
-            for xc in range(CHUNKS):
-                x_f32 = stage.tile([P, BLOCKS, BANK], F32, name=f"x_f32_{xc}")
-                nc.sync.dma_start(x_f32[:], x[:, xc * BANK : (xc + 1) * BANK].rearrange("(kb p) t -> p kb t", p=P))
-                nc.vector.tensor_copy(x_bf[xc][:], x_f32[:])
 
         identity = held.tile([P, P], BF16, name="identity")
         masks.make_identity(nc, identity[:])
@@ -82,27 +72,47 @@ def tile_cantorattention_b_kernel(tc, x, wqkv, bq, bv, wout, bout, offs, out):
             stacked[:].unsqueeze(2).to_broadcast([ROWS, CHUNK_COLS, HEAD_DIM]),
         )
 
+        w_key = load_weights(nc.sync, "w_key", wqkv[:, DIM : 2 * DIM])
+        w_q = load_weights(nc.scalar, "w_q", wqkv[:, 0:DIM])
+        bias_q = load_bias("bias_q", bq)
+        x_bf = [held.tile([P, BLOCKS, BANK], BF16, name=f"x_bf{xc}") for xc in range(CHUNKS)]
+        with tc.tile_pool(name="stage", bufs=1) as stage:
+            for xc in range(CHUNKS):
+                x_f32 = stage.tile([P, BLOCKS, BANK], F32, name=f"x_f32_{xc}")
+                nc.sync.dma_start(x_f32[:], x[:, xc * BANK : (xc + 1) * BANK].rearrange("(kb p) t -> p kb t", p=P))
+                for kb in range(BLOCKS):
+                    nc.vector.tensor_copy(x_bf[xc][:, kb, :], x_f32[:, kb, :])
+        w_val = load_weights(nc.sync, "w_val", wqkv[:, 2 * DIM : 3 * DIM])
+        bias_v = load_bias("bias_v", bv)
+        w_out = load_weights(nc.sync, "w_out", wout)
+        bias_out = load_bias("bias_out", bout)
+
+        key, q, val, scores, exps, p_rows, p_of = {}, {}, {}, {}, {}, {}, {}
         att = [held.tile([P, TOKENS], BF16, name=f"att{b}") for b in range(BLOCKS)]
 
-        def project(name, w, b, bias):
-            table = tables.tile([P, TOKENS], F32, name=name)
-            for xc in range(CHUNKS):
-                acc = psum.tile([P, BANK], F32, name="acc", bufs=3)
-                for kb in range(BLOCKS):
-                    nc.tensor.matmul(
-                        acc[:],
-                        lhsT=w[:, kb, b * P : (b + 1) * P],
-                        rhs=x_bf[xc][:, kb, :],
-                        start=(kb == 0),
-                        stop=(kb == BLOCKS - 1),
-                    )
-                if bias is None:
-                    nc.scalar.copy(table[:, xc * BANK : (xc + 1) * BANK], acc[:])
-                else:
-                    nc.scalar.activation(
-                        table[:, xc * BANK : (xc + 1) * BANK], acc[:], ACT.Identity, bias=bias[:, b : b + 1]
-                    )
-            return table
+        def project_ahead(b, xc):
+            for table, name, w, bias, block in (
+                (key, "key", w_key, None, b + 2),
+                (q, "q", w_q, bias_q, b + 2),
+                (val, "val", w_val, bias_v, b + 1),
+            ):
+                if 0 <= block < BLOCKS:
+                    if xc == 0:
+                        table[block] = tables.tile([P, TOKENS], F32, name=name)
+                    acc = psum.tile([P, BANK], F32, name="acc", bufs=BLOCKS)
+                    for kb in range(BLOCKS):
+                        nc.tensor.matmul(
+                            acc[:],
+                            lhsT=w[:, kb, block * P : (block + 1) * P],
+                            rhs=x_bf[xc][:, kb, :],
+                            start=(kb == 0),
+                            stop=(kb == BLOCKS - 1),
+                        )
+                    columns = table[block][:, xc * BANK : (xc + 1) * BANK]
+                    if bias is None:
+                        nc.scalar.copy(columns, acc[:])
+                    else:
+                        nc.scalar.activation(columns, acc[:], ACT.Identity, bias=bias[:, block : block + 1])
 
         def over_routes(small):
             return small[:].unsqueeze(2).to_broadcast([P, GROUPS, ROUTES, BLOCK_HEADS])
@@ -110,99 +120,127 @@ def tile_cantorattention_b_kernel(tc, x, wqkv, bq, bv, wout, bout, offs, out):
         def by_chunk(columns):
             return columns[:].rearrange("p (xc g) r h -> p xc (g r h)", xc=CHUNKS)
 
-        with tc.tile_pool(name="late", bufs=2) as late:
-            for b in range(BLOCKS):
-                key = project("key", w_key, b, None)
-                q = project("q", w_q, b, bias_q)
-                val = project("val", w_val, b, bias_v)
+        def softmax_exp(b):
+            top = soft.tile([P, GROUPS, BLOCK_HEADS], F32, name="top")
+            nc.vector.tensor_reduce(out=top[:], in_=scores[b][:].rearrange("p g r h -> p g h r"), axis=AXIS.X, op=ALU.max)
+            shifted = soft.tile([P, GROUPS, ROUTES, BLOCK_HEADS], F32, name="shifted")
+            nc.vector.tensor_tensor(shifted[:], scores[b][:], over_routes(top), ALU.subtract)
+            exps[b] = soft.tile([P, GROUPS, ROUTES, BLOCK_HEADS], F32, name="exps")
+            nc.scalar.activation(exps[b][:], shifted[:], ACT.Exp, scale=SCALE)
 
-                scores = psum.tile([P, GROUPS, ROUTES, BLOCK_HEADS], F32, name="scores")
+        def softmax_divide(b):
+            total = soft.tile([P, GROUPS, BLOCK_HEADS], F32, name="total")
+            nc.vector.tensor_reduce(out=total[:], in_=exps[b][:].rearrange("p g r h -> p g h r"), axis=AXIS.X, op=ALU.add)
+            inverse = soft.tile([P, GROUPS, BLOCK_HEADS], F32, name="inverse")
+            nc.vector.reciprocal(inverse[:], total[:])
+            prob = soft.tile([P, GROUPS, ROUTES, BLOCK_HEADS], F32, name="prob")
+            nc.vector.tensor_tensor(prob[:], exps[b][:], over_routes(inverse), ALU.mult)
+            parts = soft.tile([P, CHUNKS, PARTS, CHUNK_COLS], BF16, name="parts")
+            rest = soft.tile([P, GROUPS, ROUTES, BLOCK_HEADS], F32, name="rest")
+            nc.vector.tensor_copy(parts[:, :, 0, :], by_chunk(prob))
+            nc.vector.tensor_tensor(by_chunk(rest), by_chunk(prob), parts[:, :, 0, :], ALU.subtract)
+            nc.vector.tensor_copy(parts[:, :, 1, :], by_chunk(rest))
+            nc.vector.tensor_tensor(parts[:, :, 2, :], by_chunk(rest), parts[:, :, 1, :], ALU.subtract)
+            rows_psum = psum.tile([ROWS, CHUNKS * P], BF16, name="rows_psum", bufs=1)
+            for xc in range(CHUNKS):
+                nc.tensor.transpose(
+                    rows_psum[:, xc * P : (xc + 1) * P], parts[:, xc, :, :].rearrange("p k c -> p (k c)"), identity[:]
+                )
+            p_rows[b] = soft.tile([ROWS, CHUNKS * P], BF16, name="p_rows")
+            nc.scalar.copy(p_rows[b][:], rows_psum[:])
+
+        with tc.tile_pool(name="late", bufs=2) as late:
+
+            def make_p(b, unit):
+                p_of[b, unit] = late.tile([P, TOKENS], F32, name="p_block", bufs=3)
+                for i in range(ROUTES):
+                    r, xc = (unit, i) if b < LAST else (i, unit)
+                    p_psum = psum.tile([P, BANK], F32, name="p_psum")
+                    for g in range(CHUNK_GROUPS):
+                        nc.tensor.matmul(
+                            p_psum[:, g * P : (g + 1) * P],
+                            lhsT=spread[:, g, r, :],
+                            rhs=p_rows[b][:, xc * P : (xc + 1) * P],
+                            start=True,
+                            stop=True,
+                        )
+                    nc.scalar.copy(p_of[b, unit][:, i * BANK : (i + 1) * BANK], p_psum[:])
+
+            def softmax_step(b, slot):
+                if slot == 0:
+                    softmax_exp(b)
+                elif slot == 1:
+                    softmax_divide(b)
+                elif slot == 2:
+                    make_p(b, 0)
+
+            def scores_phase(b, ahead, riding):
                 for r in range(ROUTES):
-                    first_col = r * TOKENS // LIST_COLS
                     prod = ring.tile([P, TOKENS], F32, name="prod")
-                    nc.vector.tensor_tensor(
-                        prod[:], key[:].indirect(offsets[:, first_col : first_col + TOKENS // LIST_COLS]), q[:], ALU.mult
-                    )
+                    nc.vector.tensor_tensor(prod[:], key[b][:].indirect(route_offsets(r, 0, TOKENS)), q[b][:], ALU.mult)
+                    if ahead is not None:
+                        project_ahead(ahead, r)
+                    if riding is not None:
+                        softmax_step(riding, r)
+                    if r == 0:
+                        scores[b] = psum.tile([P, GROUPS, ROUTES, BLOCK_HEADS], F32, name="scores", bufs=1)
                     prod_bf = ring.tile([P, TOKENS], BF16, name="prod_bf")
                     nc.scalar.copy(prod_bf[:], prod[:])
                     for g in range(GROUPS):
                         nc.tensor.matmul(
-                            scores[:, g, r, :], lhsT=prod_bf[:, g * P : (g + 1) * P], rhs=head_of[:], start=True, stop=True
+                            scores[b][:, g, r, :], lhsT=prod_bf[:, g * P : (g + 1) * P], rhs=head_of[:], start=True, stop=True
                         )
 
-                top = soft.tile([P, GROUPS, BLOCK_HEADS], F32, name="top")
-                nc.vector.tensor_reduce(out=top[:], in_=scores[:].rearrange("p g r h -> p g h r"), axis=AXIS.X, op=ALU.max)
-                shifted = soft.tile([P, GROUPS, ROUTES, BLOCK_HEADS], F32, name="shifted")
-                nc.vector.tensor_tensor(shifted[:], scores[:], over_routes(top), ALU.subtract)
-                exps = soft.tile([P, GROUPS, ROUTES, BLOCK_HEADS], F32, name="exps")
-                nc.scalar.activation(exps[:], shifted[:], ACT.Exp, scale=SCALE)
-                total = soft.tile([P, GROUPS, BLOCK_HEADS], F32, name="total")
-                nc.vector.tensor_reduce(out=total[:], in_=exps[:].rearrange("p g r h -> p g h r"), axis=AXIS.X, op=ALU.add)
-                inverse = soft.tile([P, GROUPS, BLOCK_HEADS], F32, name="inverse")
-                nc.vector.reciprocal(inverse[:], total[:])
-                prob = soft.tile([P, GROUPS, ROUTES, BLOCK_HEADS], F32, name="prob")
-                nc.vector.tensor_tensor(prob[:], exps[:], over_routes(inverse), ALU.mult)
+            def add_route(b, r, first, count, p_columns, summed):
+                weighted = late.tile([P, count], F32, name="weighted")
+                nc.vector.tensor_tensor(
+                    weighted[:], val[b][:].indirect(route_offsets(r, first, count)), p_columns, ALU.mult
+                )
+                if r == 0:
+                    return weighted[:]
+                if r < ROUTES - 1:
+                    longer = late.tile([P, count], F32, name="longer")[:]
+                else:
+                    longer = att[b][:, first : first + count]
+                nc.vector.tensor_tensor(longer, summed, weighted[:], ALU.add)
+                return longer
 
-                parts = soft.tile([P, CHUNKS, PARTS, CHUNK_COLS], BF16, name="parts")
-                rest = soft.tile([P, GROUPS, ROUTES, BLOCK_HEADS], F32, name="rest")
-                nc.vector.tensor_copy(parts[:, :, 0, :], by_chunk(prob))
-                nc.vector.tensor_tensor(by_chunk(rest), by_chunk(prob), parts[:, :, 0, :], ALU.subtract)
-                nc.vector.tensor_copy(parts[:, :, 1, :], by_chunk(rest))
-                nc.vector.tensor_tensor(parts[:, :, 2, :], by_chunk(rest), parts[:, :, 1, :], ALU.subtract)
-
-                rows_psum = psum.tile([ROWS, CHUNKS * P], BF16, name="rows_psum", bufs=1)
-                for xc in range(CHUNKS):
-                    nc.tensor.transpose(
-                        rows_psum[:, xc * P : (xc + 1) * P], parts[:, xc, :, :].rearrange("p k c -> p (k c)"), identity[:]
-                    )
-                p_rows = soft.tile([ROWS, CHUNKS * P], BF16, name="p_rows")
-                nc.scalar.copy(p_rows[:], rows_psum[:])
-
-                span = TOKENS if b < BLOCKS - 1 else BANK
-                for first in range(0, TOKENS, span):
-                    for r in range(ROUTES):
-                        p_block = late.tile([P, span], F32, name="p_block")
-                        for at in range(0, span, BANK):
-                            xc = (first + at) // BANK
-                            p_psum = psum.tile([P, BANK], F32, name="p_psum")
-                            for g in range(CHUNK_GROUPS):
-                                nc.tensor.matmul(
-                                    p_psum[:, g * P : (g + 1) * P],
-                                    lhsT=spread[:, g, r, :],
-                                    rhs=p_rows[:, xc * P : (xc + 1) * P],
-                                    start=True,
-                                    stop=True,
-                                )
-                            nc.scalar.copy(p_block[:, at : at + BANK], p_psum[:])
-                        first_col = (r * TOKENS + first) // LIST_COLS
-                        weighted = late.tile([P, span], F32, name="weighted")
-                        nc.vector.tensor_tensor(
-                            weighted[:],
-                            val[:].indirect(offsets[:, first_col : first_col + span // LIST_COLS]),
-                            p_block[:],
-                            ALU.mult,
+            def project_out(xc):
+                accs = [psum.tile([P, BANK], F32, name="acc", bufs=BLOCKS) for ob in range(BLOCKS)]
+                for kb in range(BLOCKS):
+                    for ob in range(BLOCKS):
+                        nc.tensor.matmul(
+                            accs[ob][:],
+                            lhsT=w_out[:, kb, ob * P : (ob + 1) * P],
+                            rhs=att[kb][:, xc * BANK : (xc + 1) * BANK],
+                            start=(kb == 0),
+                            stop=(kb == BLOCKS - 1),
                         )
-                        if r == 0:
-                            summed = weighted[:]
-                        else:
-                            if r < ROUTES - 1:
-                                longer = late.tile([P, span], F32, name="longer")[:]
-                            else:
-                                longer = att[b][:, first : first + span]
-                            nc.vector.tensor_tensor(longer, summed, weighted[:], ALU.add)
-                            summed = longer
+                for ob in range(BLOCKS):
+                    result = late.tile([P, BANK], F32, name="result", bufs=BLOCKS)
+                    nc.scalar.activation(result[:], accs[ob][:], ACT.Identity, bias=bias_out[:, ob : ob + 1])
+                    nc.sync.dma_start(out[ob * P : (ob + 1) * P, xc * BANK : (xc + 1) * BANK], result[:])
 
-                    if b == BLOCKS - 1:
-                        for ob in range(BLOCKS):
-                            acc = psum.tile([P, BANK], F32, name="acc", bufs=3)
-                            for kb in range(BLOCKS):
-                                nc.tensor.matmul(
-                                    acc[:],
-                                    lhsT=w_out[:, kb, ob * P : (ob + 1) * P],
-                                    rhs=att[kb][:, first : first + BANK],
-                                    start=(kb == 0),
-                                    stop=(kb == BLOCKS - 1),
-                                )
-                            result = late.tile([P, BANK], F32, name="result")
-                            nc.scalar.activation(result[:], acc[:], ACT.Identity, bias=bias_out[:, ob : ob + 1])
-                            nc.sync.dma_start(out[ob * P : (ob + 1) * P, first : first + BANK], result[:])
+            for xc in range(CHUNKS):
+                project_ahead(-2, xc)
+            scores_phase(0, ahead=-1, riding=None)
+            scores_phase(1, ahead=None, riding=0)
+            for b in range(LAST):
+                summed = None
+                for r in range(ROUTES):
+                    summed = add_route(b, r, 0, TOKENS, p_of[b, r][:], summed)
+                    if r + 1 < ROUTES:
+                        make_p(b, r + 1)
+                    project_ahead(b, r)
+                    softmax_step(b + 1, r)
+                if b + 2 < BLOCKS:
+                    scores_phase(b + 2, ahead=None, riding=None)
+            for xc in range(CHUNKS):
+                if xc + 1 < CHUNKS:
+                    make_p(LAST, xc + 1)
+                if xc > 0:
+                    project_out(xc - 1)
+                summed = None
+                for r in range(ROUTES):
+                    summed = add_route(LAST, r, xc * BANK, BANK, p_of[LAST, xc][:, r * BANK : (r + 1) * BANK], summed)
+            project_out(CHUNKS - 1)

@@ -23,6 +23,7 @@ CHUNK_COLS = CHUNK_GROUPS * ROUTES * BLOCK_HEADS
 PARTS = 3
 ROWS = PARTS * CHUNK_COLS
 LIST_COLS = 16
+AHEAD_PER_GATHER = 2
 
 FLOPS = 2 * DIM * 3 * DIM * TOKENS + 2 * DIM * DIM * TOKENS + 4 * DIM * ROUTES * TOKENS
 
@@ -87,32 +88,31 @@ def tile_cantorattention_b_kernel(tc, x, wqkv, bq, bv, wout, bout, offs, out):
         w_out = load_weights(nc.sync, "w_out", wout)
         bias_out = load_bias("bias_out", bout)
 
-        key, q, val, scores, exps, p_rows, p_of = {}, {}, {}, {}, {}, {}, {}
+        table, scores, exps, parts, p_rows, p_of = {}, {}, {}, {}, {}, {}
         att = [held.tile([P, TOKENS], BF16, name=f"att{b}") for b in range(BLOCKS)]
+        weights_of = {"key": w_key, "q": w_q, "val": w_val}
+        bias_of = {"key": None, "q": bias_q, "val": bias_v}
 
-        def project_ahead(b, xc):
-            for table, name, w, bias, block in (
-                (key, "key", w_key, None, b + 2),
-                (q, "q", w_q, bias_q, b + 2),
-                (val, "val", w_val, bias_v, b + 1),
-            ):
-                if 0 <= block < BLOCKS:
-                    if xc == 0:
-                        table[block] = tables.tile([P, TOKENS], F32, name=name)
-                    acc = psum.tile([P, BANK], F32, name="acc", bufs=BLOCKS)
-                    for kb in range(BLOCKS):
-                        nc.tensor.matmul(
-                            acc[:],
-                            lhsT=w[:, kb, block * P : (block + 1) * P],
-                            rhs=x_bf[xc][:, kb, :],
-                            start=(kb == 0),
-                            stop=(kb == BLOCKS - 1),
-                        )
-                    columns = table[block][:, xc * BANK : (xc + 1) * BANK]
-                    if bias is None:
-                        nc.scalar.copy(columns, acc[:])
-                    else:
-                        nc.scalar.activation(columns, acc[:], ACT.Identity, bias=bias[:, block : block + 1])
+        def project_sums(name, b, xc):
+            acc = psum.tile([P, BANK], F32, name="acc", bufs=BLOCKS)
+            for kb in range(BLOCKS):
+                nc.tensor.matmul(
+                    acc[:],
+                    lhsT=weights_of[name][:, kb, b * P : (b + 1) * P],
+                    rhs=x_bf[xc][:, kb, :],
+                    start=(kb == 0),
+                    stop=(kb == BLOCKS - 1),
+                )
+            return acc
+
+        def store_sums(name, b, xc, acc):
+            if xc == 0:
+                table[name, b] = tables.tile([P, TOKENS], F32, name=name)
+            columns = table[name, b][:, xc * BANK : (xc + 1) * BANK]
+            if bias_of[name] is None:
+                nc.scalar.copy(columns, acc[:])
+            else:
+                nc.scalar.activation(columns, acc[:], ACT.Identity, bias=bias_of[name][:, b : b + 1])
 
         def over_routes(small):
             return small[:].unsqueeze(2).to_broadcast([P, GROUPS, ROUTES, BLOCK_HEADS])
@@ -135,36 +135,30 @@ def tile_cantorattention_b_kernel(tc, x, wqkv, bq, bv, wout, bout, offs, out):
             nc.vector.reciprocal(inverse[:], total[:])
             prob = soft.tile([P, GROUPS, ROUTES, BLOCK_HEADS], F32, name="prob")
             nc.vector.tensor_tensor(prob[:], exps[b][:], over_routes(inverse), ALU.mult)
-            parts = soft.tile([P, CHUNKS, PARTS, CHUNK_COLS], BF16, name="parts")
+            parts[b] = soft.tile([P, CHUNKS, PARTS, CHUNK_COLS], BF16, name="parts")
             rest = soft.tile([P, GROUPS, ROUTES, BLOCK_HEADS], F32, name="rest")
-            nc.vector.tensor_copy(parts[:, :, 0, :], by_chunk(prob))
-            nc.vector.tensor_tensor(by_chunk(rest), by_chunk(prob), parts[:, :, 0, :], ALU.subtract)
-            nc.vector.tensor_copy(parts[:, :, 1, :], by_chunk(rest))
-            nc.vector.tensor_tensor(parts[:, :, 2, :], by_chunk(rest), parts[:, :, 1, :], ALU.subtract)
+            nc.vector.tensor_copy(parts[b][:, :, 0, :], by_chunk(prob))
+            nc.vector.tensor_tensor(by_chunk(rest), by_chunk(prob), parts[b][:, :, 0, :], ALU.subtract)
+            nc.vector.tensor_copy(parts[b][:, :, 1, :], by_chunk(rest))
+            nc.vector.tensor_tensor(parts[b][:, :, 2, :], by_chunk(rest), parts[b][:, :, 1, :], ALU.subtract)
+
+        def transpose_parts(b):
             rows_psum = psum.tile([ROWS, CHUNKS * P], BF16, name="rows_psum", bufs=1)
             for xc in range(CHUNKS):
                 nc.tensor.transpose(
-                    rows_psum[:, xc * P : (xc + 1) * P], parts[:, xc, :, :].rearrange("p k c -> p (k c)"), identity[:]
+                    rows_psum[:, xc * P : (xc + 1) * P], parts[b][:, xc, :, :].rearrange("p k c -> p (k c)"), identity[:]
                 )
             p_rows[b] = soft.tile([ROWS, CHUNKS * P], BF16, name="p_rows")
             nc.scalar.copy(p_rows[b][:], rows_psum[:])
 
         with tc.tile_pool(name="late", bufs=2) as late:
 
-            def make_p(b, unit):
-                p_of[b, unit] = late.tile([P, TOKENS], F32, name="p_block", bufs=3)
-                for i in range(ROUTES):
-                    r, xc = (unit, i) if b < LAST else (i, unit)
-                    p_psum = psum.tile([P, BANK], F32, name="p_psum")
-                    for g in range(CHUNK_GROUPS):
-                        nc.tensor.matmul(
-                            p_psum[:, g * P : (g + 1) * P],
-                            lhsT=spread[:, g, r, :],
-                            rhs=p_rows[b][:, xc * P : (xc + 1) * P],
-                            start=True,
-                            stop=True,
-                        )
-                    nc.scalar.copy(p_of[b, unit][:, i * BANK : (i + 1) * BANK], p_psum[:])
+            def make_p(b, r):
+                p_of[b, r] = late.tile([P, CHUNKS, CHUNK_GROUPS, P], F32, name="p_block", bufs=ROUTES)
+                for g in range(CHUNK_GROUPS):
+                    p_psum = psum.tile([P, CHUNKS * P], F32, name="p_psum")
+                    nc.tensor.matmul(p_psum[:], lhsT=spread[:, g, r, :], rhs=p_rows[b][:], start=True, stop=True)
+                    nc.scalar.copy(p_of[b, r][:, :, g, :], p_psum[:].rearrange("p (xc i) -> p xc i", xc=CHUNKS))
 
             def softmax_step(b, slot):
                 if slot == 0:
@@ -172,29 +166,47 @@ def tile_cantorattention_b_kernel(tc, x, wqkv, bq, bv, wout, bout, offs, out):
                 elif slot == 1:
                     softmax_divide(b)
                 elif slot == 2:
+                    transpose_parts(b)
                     make_p(b, 0)
+                else:
+                    make_p(b, 1)
 
-            def scores_phase(b, ahead, riding):
-                for r in range(ROUTES):
-                    prod = ring.tile([P, TOKENS], F32, name="prod")
-                    nc.vector.tensor_tensor(prod[:], key[b][:].indirect(route_offsets(r, 0, TOKENS)), q[b][:], ALU.mult)
-                    if ahead is not None:
-                        project_ahead(ahead, r)
-                    if riding is not None:
-                        softmax_step(riding, r)
-                    if r == 0:
-                        scores[b] = psum.tile([P, GROUPS, ROUTES, BLOCK_HEADS], F32, name="scores", bufs=1)
-                    prod_bf = ring.tile([P, TOKENS], BF16, name="prod_bf")
-                    nc.scalar.copy(prod_bf[:], prod[:])
-                    for g in range(GROUPS):
+            def sum_heads(b, r, prod):
+                prod_bf = ring.tile([P, TOKENS], BF16, name="prod_bf")
+                for xc in range(CHUNKS):
+                    nc.scalar.copy(prod_bf[:, xc * BANK : (xc + 1) * BANK], prod[:, xc * BANK : (xc + 1) * BANK])
+                    for g in range(xc * CHUNK_GROUPS, (xc + 1) * CHUNK_GROUPS):
                         nc.tensor.matmul(
                             scores[b][:, g, r, :], lhsT=prod_bf[:, g * P : (g + 1) * P], rhs=head_of[:], start=True, stop=True
                         )
 
+            def scores_phase(b, ahead, riding):
+                previous = None
+                for r in range(ROUTES):
+                    prod = ring.tile([P, TOKENS], F32, name="prod")
+                    nc.vector.tensor_tensor(
+                        prod[:], table["key", b][:].indirect(route_offsets(r, 0, TOKENS)), table["q", b][:], ALU.mult
+                    )
+                    now = ahead[AHEAD_PER_GATHER * r : AHEAD_PER_GATHER * (r + 1)]
+                    accs = [project_sums(name, block, xc) for name, block, xc in now]
+                    if r > 0:
+                        sum_heads(b, r - 1, previous)
+                    for (name, block, xc), acc in zip(now, accs):
+                        store_sums(name, block, xc, acc)
+                    if riding is not None:
+                        softmax_step(riding, r)
+                    if r == 0:
+                        scores[b] = psum.tile([P, GROUPS, ROUTES, BLOCK_HEADS], F32, name="scores", bufs=1)
+                    previous = prod
+                sum_heads(b, ROUTES - 1, previous)
+
             def add_route(b, r, first, count, p_columns, summed):
                 weighted = late.tile([P, count], F32, name="weighted")
                 nc.vector.tensor_tensor(
-                    weighted[:], val[b][:].indirect(route_offsets(r, first, count)), p_columns, ALU.mult
+                    weighted[:],
+                    table["val", b][:].indirect(route_offsets(r, first, count)),
+                    p_columns,
+                    ALU.mult,
                 )
                 if r == 0:
                     return weighted[:]
@@ -222,25 +234,27 @@ def tile_cantorattention_b_kernel(tc, x, wqkv, bq, bv, wout, bout, offs, out):
                     nc.sync.dma_start(out[ob * P : (ob + 1) * P, xc * BANK : (xc + 1) * BANK], result[:])
 
             for xc in range(CHUNKS):
-                project_ahead(-2, xc)
-            scores_phase(0, ahead=-1, riding=None)
-            scores_phase(1, ahead=None, riding=0)
+                for name in ("key", "q"):
+                    store_sums(name, 0, xc, project_sums(name, 0, xc))
+            scores_phase(0, ahead=[(name, 1, xc) for xc in range(CHUNKS) for name in ("key", "q")], riding=None)
+            scores_phase(1, ahead=[("val", 0, xc) for xc in range(CHUNKS)], riding=0)
             for b in range(LAST):
                 summed = None
                 for r in range(ROUTES):
-                    summed = add_route(b, r, 0, TOKENS, p_of[b, r][:], summed)
-                    if r + 1 < ROUTES:
-                        make_p(b, r + 1)
-                    project_ahead(b, r)
+                    summed = add_route(b, r, 0, TOKENS, p_of[b, r][:].rearrange("p xc g i -> p (xc g i)"), summed)
+                    if r + 2 < ROUTES:
+                        make_p(b, r + 2)
+                    for name, block in (("key", b + 2), ("q", b + 2), ("val", b + 1)):
+                        if block < BLOCKS:
+                            store_sums(name, block, r, project_sums(name, block, r))
                     softmax_step(b + 1, r)
                 if b + 2 < BLOCKS:
-                    scores_phase(b + 2, ahead=None, riding=None)
+                    scores_phase(b + 2, ahead=[], riding=None)
+            make_p(LAST, 2)
+            make_p(LAST, 3)
             for xc in range(CHUNKS):
-                if xc + 1 < CHUNKS:
-                    make_p(LAST, xc + 1)
-                if xc > 0:
-                    project_out(xc - 1)
                 summed = None
                 for r in range(ROUTES):
-                    summed = add_route(LAST, r, xc * BANK, BANK, p_of[LAST, xc][:, r * BANK : (r + 1) * BANK], summed)
-            project_out(CHUNKS - 1)
+                    p_columns = p_of[LAST, r][:, xc, :, :].rearrange("p g i -> p (g i)")
+                    summed = add_route(LAST, r, xc * BANK, BANK, p_columns, summed)
+                project_out(xc)

@@ -14,16 +14,18 @@ HEAD_DIM = 64
 SCALE = 0.125
 BLOCKS = DIM // P
 LAST = BLOCKS - 1
+PAIR = 2
 BLOCK_HEADS = P // HEAD_DIM
 BANK = 512
 CHUNKS = TOKENS // BANK
 GROUPS = TOKENS // P
+PAIR_GROUPS = PAIR * GROUPS
+PAIR_CHUNKS = PAIR * CHUNKS
 CHUNK_GROUPS = BANK // P
 CHUNK_COLS = CHUNK_GROUPS * ROUTES * BLOCK_HEADS
 PARTS = 3
 ROWS = PARTS * CHUNK_COLS
 LIST_COLS = 16
-AHEAD_PER_GATHER = 2
 
 FLOPS = 2 * DIM * 3 * DIM * TOKENS + 2 * DIM * DIM * TOKENS + 4 * DIM * ROUTES * TOKENS
 
@@ -43,6 +45,18 @@ def tile_cantorattention_b_kernel(tc, x, wqkv, bq, bv, wout, bout, offs, out):
         def route_offsets(r, first, count):
             column = (r * TOKENS + first) // LIST_COLS
             return offsets[:, column : column + count // LIST_COLS]
+
+        waiting = {"add": None}
+
+        def add_waiting():
+            if waiting["add"] is not None:
+                longer, summed, weighted = waiting["add"]
+                nc.vector.tensor_tensor(longer, summed, weighted, ALU.add)
+                waiting["add"] = None
+
+        def gather_times(product, window, r, first, count, other):
+            nc.vector.tensor_tensor(product, window[:].indirect(route_offsets(r, first, count)), other, ALU.mult)
+            add_waiting()
 
         def load_weights(queue, name, columns):
             w = held.tile([P, BLOCKS, DIM], BF16, name=name)
@@ -88,10 +102,11 @@ def tile_cantorattention_b_kernel(tc, x, wqkv, bq, bv, wout, bout, offs, out):
         w_out = load_weights(nc.sync, "w_out", wout)
         bias_out = load_bias("bias_out", bout)
 
-        table, scores, exps, parts, p_rows, p_of = {}, {}, {}, {}, {}, {}
+        table, top, exps, prob, parts, rest, p_rows, p_of = {}, {}, {}, {}, {}, {}, {}, {}
         att = [held.tile([P, TOKENS], BF16, name=f"att{b}") for b in range(BLOCKS)]
         weights_of = {"key": w_key, "q": w_q, "val": w_val}
         bias_of = {"key": None, "q": bias_q, "val": bias_v}
+        scores = psum.tile([P, BLOCKS * GROUPS, ROUTES, BLOCK_HEADS], F32, name="scores", bufs=1)
 
         def project_sums(name, b, xc):
             acc = psum.tile([P, BANK], F32, name="acc", bufs=BLOCKS)
@@ -114,107 +129,86 @@ def tile_cantorattention_b_kernel(tc, x, wqkv, bq, bv, wout, bout, offs, out):
             else:
                 nc.scalar.activation(columns, acc[:], ACT.Identity, bias=bias_of[name][:, b : b + 1])
 
+        def small_tile(name):
+            return soft.tile([P, PAIR_GROUPS, BLOCK_HEADS], F32, name=name)
+
+        def full_tile(name):
+            return soft.tile([P, PAIR_GROUPS, ROUTES, BLOCK_HEADS], F32, name=name)
+
+        def routes_last(columns):
+            return columns.rearrange("p g r h -> p g h r")
+
         def over_routes(small):
-            return small[:].unsqueeze(2).to_broadcast([P, GROUPS, ROUTES, BLOCK_HEADS])
+            return small[:].unsqueeze(2).to_broadcast([P, PAIR_GROUPS, ROUTES, BLOCK_HEADS])
 
         def by_chunk(columns):
-            return columns[:].rearrange("p (xc g) r h -> p xc (g r h)", xc=CHUNKS)
+            return columns[:].rearrange("p (c g) r h -> p c (g r h)", c=PAIR_CHUNKS)
 
-        def softmax_exp(b):
-            top = soft.tile([P, GROUPS, BLOCK_HEADS], F32, name="top")
-            nc.vector.tensor_reduce(out=top[:], in_=scores[b][:].rearrange("p g r h -> p g h r"), axis=AXIS.X, op=ALU.max)
-            shifted = soft.tile([P, GROUPS, ROUTES, BLOCK_HEADS], F32, name="shifted")
-            nc.vector.tensor_tensor(shifted[:], scores[b][:], over_routes(top), ALU.subtract)
-            exps[b] = soft.tile([P, GROUPS, ROUTES, BLOCK_HEADS], F32, name="exps")
-            nc.scalar.activation(exps[b][:], shifted[:], ACT.Exp, scale=SCALE)
-
-        def softmax_divide(b):
-            total = soft.tile([P, GROUPS, BLOCK_HEADS], F32, name="total")
-            nc.vector.tensor_reduce(out=total[:], in_=exps[b][:].rearrange("p g r h -> p g h r"), axis=AXIS.X, op=ALU.add)
-            inverse = soft.tile([P, GROUPS, BLOCK_HEADS], F32, name="inverse")
-            nc.vector.reciprocal(inverse[:], total[:])
-            prob = soft.tile([P, GROUPS, ROUTES, BLOCK_HEADS], F32, name="prob")
-            nc.vector.tensor_tensor(prob[:], exps[b][:], over_routes(inverse), ALU.mult)
-            parts[b] = soft.tile([P, CHUNKS, PARTS, CHUNK_COLS], BF16, name="parts")
-            rest = soft.tile([P, GROUPS, ROUTES, BLOCK_HEADS], F32, name="rest")
-            nc.vector.tensor_copy(parts[b][:, :, 0, :], by_chunk(prob))
-            nc.vector.tensor_tensor(by_chunk(rest), by_chunk(prob), parts[b][:, :, 0, :], ALU.subtract)
-            nc.vector.tensor_copy(parts[b][:, :, 1, :], by_chunk(rest))
-            nc.vector.tensor_tensor(parts[b][:, :, 2, :], by_chunk(rest), parts[b][:, :, 1, :], ALU.subtract)
-
-        def transpose_parts(b):
-            rows_psum = psum.tile([ROWS, CHUNKS * P], BF16, name="rows_psum", bufs=1)
-            for xc in range(CHUNKS):
-                nc.tensor.transpose(
-                    rows_psum[:, xc * P : (xc + 1) * P], parts[b][:, xc, :, :].rearrange("p k c -> p (k c)"), identity[:]
-                )
-            p_rows[b] = soft.tile([ROWS, CHUNKS * P], BF16, name="p_rows")
-            nc.scalar.copy(p_rows[b][:], rows_psum[:])
+        def softmax_step(pair, step):
+            pair_scores = scores[:, pair * PAIR_GROUPS : (pair + 1) * PAIR_GROUPS, :, :]
+            if step == 0:
+                top[pair] = small_tile("top")
+                nc.vector.tensor_reduce(out=top[pair][:], in_=routes_last(pair_scores), axis=AXIS.X, op=ALU.max)
+            elif step == 1:
+                shifted = full_tile("shifted")
+                nc.vector.tensor_tensor(shifted[:], pair_scores, over_routes(top[pair]), ALU.subtract)
+                exps[pair] = full_tile("exps")
+                nc.scalar.activation(exps[pair][:], shifted[:], ACT.Exp, scale=SCALE)
+            elif step == 2:
+                total = small_tile("total")
+                nc.vector.tensor_reduce(out=total[:], in_=routes_last(exps[pair][:]), axis=AXIS.X, op=ALU.add)
+                inverse = small_tile("inverse")
+                nc.vector.reciprocal(inverse[:], total[:])
+                prob[pair] = full_tile("prob")
+                nc.vector.tensor_tensor(prob[pair][:], exps[pair][:], over_routes(inverse), ALU.mult)
+            elif step == 3:
+                parts[pair] = soft.tile([P, PAIR_CHUNKS, PARTS, CHUNK_COLS], BF16, name="parts")
+                rest[pair] = full_tile("rest")
+                nc.vector.tensor_copy(parts[pair][:, :, 0, :], by_chunk(prob[pair]))
+                nc.vector.tensor_tensor(by_chunk(rest[pair]), by_chunk(prob[pair]), parts[pair][:, :, 0, :], ALU.subtract)
+            elif step == 4:
+                nc.vector.tensor_copy(parts[pair][:, :, 1, :], by_chunk(rest[pair]))
+                nc.vector.tensor_tensor(parts[pair][:, :, 2, :], by_chunk(rest[pair]), parts[pair][:, :, 1, :], ALU.subtract)
+            elif step == 5:
+                rows_psum = psum.tile([ROWS, PAIR_CHUNKS * P], BF16, name="rows_psum", bufs=1)
+                for c in range(PAIR_CHUNKS):
+                    nc.tensor.transpose(
+                        rows_psum[:, c * P : (c + 1) * P], parts[pair][:, c, :, :].rearrange("p k c -> p (k c)"), identity[:]
+                    )
+                p_rows[pair] = soft.tile([ROWS, PAIR_CHUNKS * P], BF16, name="p_rows")
+                nc.scalar.copy(p_rows[pair][:], rows_psum[:])
 
         with tc.tile_pool(name="late", bufs=2) as late:
 
-            def make_p(b, r):
-                p_of[b, r] = late.tile([P, CHUNKS, CHUNK_GROUPS, P], F32, name="p_block", bufs=ROUTES)
-                for g in range(CHUNK_GROUPS):
-                    p_psum = psum.tile([P, CHUNKS * P], F32, name="p_psum")
-                    nc.tensor.matmul(p_psum[:], lhsT=spread[:, g, r, :], rhs=p_rows[b][:], start=True, stop=True)
-                    nc.scalar.copy(p_of[b, r][:, :, g, :], p_psum[:].rearrange("p (xc i) -> p xc i", xc=CHUNKS))
-
-            def softmax_step(b, slot):
-                if slot == 0:
-                    softmax_exp(b)
-                elif slot == 1:
-                    softmax_divide(b)
-                elif slot == 2:
-                    transpose_parts(b)
-                    make_p(b, 0)
-                else:
-                    make_p(b, 1)
-
-            def sum_heads(b, r, prod):
-                prod_bf = ring.tile([P, TOKENS], BF16, name="prod_bf")
-                for xc in range(CHUNKS):
-                    nc.scalar.copy(prod_bf[:, xc * BANK : (xc + 1) * BANK], prod[:, xc * BANK : (xc + 1) * BANK])
-                    for g in range(xc * CHUNK_GROUPS, (xc + 1) * CHUNK_GROUPS):
+            def make_p(unit):
+                if not 0 <= unit < BLOCKS * ROUTES:
+                    return
+                b, which = divmod(unit, ROUTES)
+                p_of[unit] = late.tile([P, TOKENS], F32, name="p_block", bufs=4)
+                for i in range(ROUTES):
+                    r, xc = (which, i) if b < LAST else (i, which)
+                    c = (b % PAIR) * CHUNKS + xc
+                    p_psum = psum.tile([P, BANK], F32, name="p_psum")
+                    for g in range(CHUNK_GROUPS):
                         nc.tensor.matmul(
-                            scores[b][:, g, r, :], lhsT=prod_bf[:, g * P : (g + 1) * P], rhs=head_of[:], start=True, stop=True
+                            p_psum[:, g * P : (g + 1) * P],
+                            lhsT=spread[:, g, r, :],
+                            rhs=p_rows[b // PAIR][:, c * P : (c + 1) * P],
+                            start=True,
+                            stop=True,
                         )
-
-            def scores_phase(b, ahead, riding):
-                previous = None
-                for r in range(ROUTES):
-                    prod = ring.tile([P, TOKENS], F32, name="prod")
-                    nc.vector.tensor_tensor(
-                        prod[:], table["key", b][:].indirect(route_offsets(r, 0, TOKENS)), table["q", b][:], ALU.mult
-                    )
-                    now = ahead[AHEAD_PER_GATHER * r : AHEAD_PER_GATHER * (r + 1)]
-                    accs = [project_sums(name, block, xc) for name, block, xc in now]
-                    if r > 0:
-                        sum_heads(b, r - 1, previous)
-                    for (name, block, xc), acc in zip(now, accs):
-                        store_sums(name, block, xc, acc)
-                    if riding is not None:
-                        softmax_step(riding, r)
-                    if r == 0:
-                        scores[b] = psum.tile([P, GROUPS, ROUTES, BLOCK_HEADS], F32, name="scores", bufs=1)
-                    previous = prod
-                sum_heads(b, ROUTES - 1, previous)
+                    nc.scalar.copy(p_of[unit][:, i * BANK : (i + 1) * BANK], p_psum[:])
 
             def add_route(b, r, first, count, p_columns, summed):
-                weighted = late.tile([P, count], F32, name="weighted")
-                nc.vector.tensor_tensor(
-                    weighted[:],
-                    table["val", b][:].indirect(route_offsets(r, first, count)),
-                    p_columns,
-                    ALU.mult,
-                )
+                weighted = late.tile([P, count], F32, name="weighted", bufs=3)
+                gather_times(weighted[:], table["val", b], r, first, count, p_columns)
                 if r == 0:
                     return weighted[:]
                 if r < ROUTES - 1:
                     longer = late.tile([P, count], F32, name="longer")[:]
                 else:
                     longer = att[b][:, first : first + count]
-                nc.vector.tensor_tensor(longer, summed, weighted[:], ALU.add)
+                waiting["add"] = (longer, summed, weighted[:])
                 return longer
 
             def project_out(xc):
@@ -233,28 +227,53 @@ def tile_cantorattention_b_kernel(tc, x, wqkv, bq, bv, wout, bout, offs, out):
                     nc.scalar.activation(result[:], accs[ob][:], ACT.Identity, bias=bias_out[:, ob : ob + 1])
                     nc.sync.dma_start(out[ob * P : (ob + 1) * P, xc * BANK : (xc + 1) * BANK], result[:])
 
+            def sum_heads(b, r, prod):
+                prod_bf = ring.tile([P, TOKENS], BF16, name="prod_bf")
+                nc.scalar.copy(prod_bf[:], prod[:])
+                for g in range(GROUPS):
+                    nc.tensor.matmul(
+                        scores[:, b * GROUPS + g, r, :], lhsT=prod_bf[:, g * P : (g + 1) * P], rhs=head_of[:], start=True, stop=True
+                    )
+
             for xc in range(CHUNKS):
                 for name in ("key", "q"):
                     store_sums(name, 0, xc, project_sums(name, 0, xc))
-            scores_phase(0, ahead=[(name, 1, xc) for xc in range(CHUNKS) for name in ("key", "q")], riding=None)
-            scores_phase(1, ahead=[("val", 0, xc) for xc in range(CHUNKS)], riding=0)
+
+            previous = None
+            for b in range(BLOCKS):
+                ahead = [("key", b + 1), ("q", b + 1)] if b < LAST else [("val", 0)]
+                for r in range(ROUTES):
+                    prod = ring.tile([P, TOKENS], F32, name="prod")
+                    gather_times(prod[:], table["key", b], r, 0, TOKENS, table["q", b][:])
+                    accs = [project_sums(name, block, r) for name, block in ahead]
+                    if previous is not None:
+                        sum_heads(*previous)
+                    for (name, block), acc in zip(ahead, accs):
+                        store_sums(name, block, r, acc)
+                    if b >= PAIR:
+                        softmax_step(0, (b - PAIR) * ROUTES + r - 1)
+                    if b == LAST:
+                        make_p(r - 2)
+                    previous = (b, r, prod)
+            sum_heads(*previous)
+
             for b in range(LAST):
                 summed = None
                 for r in range(ROUTES):
-                    summed = add_route(b, r, 0, TOKENS, p_of[b, r][:].rearrange("p xc g i -> p (xc g i)"), summed)
-                    if r + 2 < ROUTES:
-                        make_p(b, r + 2)
-                    for name, block in (("key", b + 2), ("q", b + 2), ("val", b + 1)):
-                        if block < BLOCKS:
-                            store_sums(name, block, r, project_sums(name, block, r))
-                    softmax_step(b + 1, r)
-                if b + 2 < BLOCKS:
-                    scores_phase(b + 2, ahead=[], riding=None)
-            make_p(LAST, 2)
-            make_p(LAST, 3)
+                    unit = b * ROUTES + r
+                    summed = add_route(b, r, 0, TOKENS, p_of[unit][:], summed)
+                    store_sums("val", b + 1, r, project_sums("val", b + 1, r))
+                    if b < PAIR:
+                        softmax_step(1, unit - 1)
+                    make_p(unit + 2)
+
             for xc in range(CHUNKS):
+                unit = LAST * ROUTES + xc
+                make_p(unit + 2)
                 summed = None
                 for r in range(ROUTES):
-                    p_columns = p_of[LAST, r][:, xc, :, :].rearrange("p g i -> p (g i)")
-                    summed = add_route(LAST, r, xc * BANK, BANK, p_columns, summed)
-                project_out(xc)
+                    summed = add_route(LAST, r, xc * BANK, BANK, p_of[unit][:, r * BANK : (r + 1) * BANK], summed)
+                    if r == 0 and xc > 0:
+                        project_out(xc - 1)
+            add_waiting()
+            project_out(CHUNKS - 1)

@@ -161,13 +161,13 @@ def tile_cantorattention_b_kernel(tc, x, wqkv, bq, bv, wout, bout, offs, out):
                 nc.vector.reciprocal(inverse[:], total[:])
                 prob[pair] = full_tile("prob")
                 nc.vector.tensor_tensor(prob[pair][:], exps[pair][:], over_routes(inverse), ALU.mult)
-            elif step == 3:
                 parts[pair] = soft.tile([P, PAIR_CHUNKS, PARTS, CHUNK_COLS], BF16, name="parts")
+                nc.scalar.copy(parts[pair][:, :, 0, :], by_chunk(prob[pair]))
+            elif step == 3:
                 rest[pair] = full_tile("rest")
-                nc.vector.tensor_copy(parts[pair][:, :, 0, :], by_chunk(prob[pair]))
                 nc.vector.tensor_tensor(by_chunk(rest[pair]), by_chunk(prob[pair]), parts[pair][:, :, 0, :], ALU.subtract)
+                nc.scalar.copy(parts[pair][:, :, 1, :], by_chunk(rest[pair]))
             elif step == 4:
-                nc.vector.tensor_copy(parts[pair][:, :, 1, :], by_chunk(rest[pair]))
                 nc.vector.tensor_tensor(parts[pair][:, :, 2, :], by_chunk(rest[pair]), parts[pair][:, :, 1, :], ALU.subtract)
             elif step == 5:
                 rows_psum = psum.tile([ROWS, PAIR_CHUNKS * P], BF16, name="rows_psum", bufs=1)
@@ -224,7 +224,10 @@ def tile_cantorattention_b_kernel(tc, x, wqkv, bq, bv, wout, bout, offs, out):
                         )
                 for ob in range(BLOCKS):
                     result = late.tile([P, BANK], F32, name="result", bufs=BLOCKS)
-                    nc.scalar.activation(result[:], accs[ob][:], ACT.Identity, bias=bias_out[:, ob : ob + 1])
+                    if xc == CHUNKS - 1 and ob % 2 == 1:
+                        nc.vector.tensor_scalar_add(result[:], accs[ob][:], bias_out[:, ob : ob + 1])
+                    else:
+                        nc.scalar.activation(result[:], accs[ob][:], ACT.Identity, bias=bias_out[:, ob : ob + 1])
                     nc.sync.dma_start(out[ob * P : (ob + 1) * P, xc * BANK : (xc + 1) * BANK], result[:])
 
             def sum_heads(b, r, prod):

@@ -26,6 +26,7 @@ CHUNK_COLS = CHUNK_GROUPS * ROUTES * BLOCK_HEADS
 PARTS = 3
 ROWS = PARTS * CHUNK_COLS
 LIST_COLS = 16
+TENSOR_CHUNKS = 2
 
 FLOPS = 2 * DIM * 3 * DIM * TOKENS + 2 * DIM * DIM * TOKENS + 4 * DIM * ROUTES * TOKENS
 
@@ -46,17 +47,11 @@ def tile_cantorattention_b_kernel(tc, x, wqkv, bq, bv, wout, bout, offs, out):
             column = (r * TOKENS + first) // LIST_COLS
             return offsets[:, column : column + count // LIST_COLS]
 
-        waiting = {"add": None}
-
-        def add_waiting():
-            if waiting["add"] is not None:
-                longer, summed, weighted = waiting["add"]
-                nc.vector.tensor_tensor(longer, summed, weighted, ALU.add)
-                waiting["add"] = None
+        waiting = {"sum": None}
 
         def gather_times(product, window, r, first, count, other):
             nc.vector.tensor_tensor(product, window[:].indirect(route_offsets(r, first, count)), other, ALU.mult)
-            add_waiting()
+            sum_waiting()
 
         def load_weights(queue, name, columns):
             w = held.tile([P, BLOCKS, DIM], BF16, name=name)
@@ -71,6 +66,8 @@ def tile_cantorattention_b_kernel(tc, x, wqkv, bq, bv, wout, bout, offs, out):
 
         identity = held.tile([P, P], BF16, name="identity")
         masks.make_identity(nc, identity[:])
+        identity_f32 = held.tile([P, P], F32, name="identity_f32")
+        masks.make_identity(nc, identity_f32[:])
         head_of = held.tile([P, BLOCK_HEADS], BF16, name="head_of")
         nc.vector.memset(head_of[:], 0.0)
         for h in range(BLOCK_HEADS):
@@ -104,6 +101,19 @@ def tile_cantorattention_b_kernel(tc, x, wqkv, bq, bv, wout, bout, offs, out):
 
         table, top, exps, prob, parts, rest, p_rows, p_of = {}, {}, {}, {}, {}, {}, {}, {}
         att = [held.tile([P, TOKENS], BF16, name=f"att{b}") for b in range(BLOCKS)]
+        def sum_waiting():
+            if waiting["sum"] is None:
+                return
+            b, r, first, weighted, accs, summed, longer = waiting["sum"]
+            waiting["sum"] = None
+            for xc, acc in enumerate(accs):
+                columns = slice(xc * BANK, (xc + 1) * BANK)
+                nc.tensor.matmul(acc[:], lhsT=identity_f32[:], rhs=weighted[:, columns], start=(r == 0), stop=(r == ROUTES - 1))
+                if r == ROUTES - 1:
+                    nc.scalar.copy(att[b][:, first + xc * BANK : first + (xc + 1) * BANK], acc[:])
+            if r > 0:
+                nc.vector.tensor_tensor(longer, summed, weighted[:, len(accs) * BANK :], ALU.add)
+
         weights_of = {"key": w_key, "q": w_q, "val": w_val}
         bias_of = {"key": None, "q": bias_q, "val": bias_v}
         scores = psum.tile([P, BLOCKS * GROUPS, ROUTES, BLOCK_HEADS], F32, name="scores", bufs=1)
@@ -199,16 +209,17 @@ def tile_cantorattention_b_kernel(tc, x, wqkv, bq, bv, wout, bout, offs, out):
                         )
                     nc.scalar.copy(p_of[unit][:, i * BANK : (i + 1) * BANK], p_psum[:])
 
-            def add_route(b, r, first, count, p_columns, summed):
+            def add_route(b, r, first, count, p_columns, accs, summed):
                 weighted = late.tile([P, count], F32, name="weighted", bufs=3)
                 gather_times(weighted[:], table["val", b], r, first, count, p_columns)
+                own = len(accs) * BANK
                 if r == 0:
-                    return weighted[:]
-                if r < ROUTES - 1:
-                    longer = late.tile([P, count], F32, name="longer")[:]
+                    longer = weighted[:, own:]
+                elif r < ROUTES - 1:
+                    longer = late.tile([P, count - own], F32, name="longer")[:]
                 else:
-                    longer = att[b][:, first : first + count]
-                waiting["add"] = (longer, summed, weighted[:])
+                    longer = att[b][:, first + own : first + count]
+                waiting["sum"] = (b, r, first, weighted, accs, summed, longer)
                 return longer
 
             def project_out(xc):
@@ -261,10 +272,11 @@ def tile_cantorattention_b_kernel(tc, x, wqkv, bq, bv, wout, bout, offs, out):
             sum_heads(*previous)
 
             for b in range(LAST):
+                accs = [psum.tile([P, BANK], F32, name="acc", bufs=BLOCKS) for xc in range(TENSOR_CHUNKS)]
                 summed = None
                 for r in range(ROUTES):
                     unit = b * ROUTES + r
-                    summed = add_route(b, r, 0, TOKENS, p_of[unit][:], summed)
+                    summed = add_route(b, r, 0, TOKENS, p_of[unit][:], accs, summed)
                     store_sums("val", b + 1, r, project_sums("val", b + 1, r))
                     if b < PAIR:
                         softmax_step(1, unit - 1)
@@ -275,8 +287,8 @@ def tile_cantorattention_b_kernel(tc, x, wqkv, bq, bv, wout, bout, offs, out):
                 make_p(unit + 2)
                 summed = None
                 for r in range(ROUTES):
-                    summed = add_route(LAST, r, xc * BANK, BANK, p_of[unit][:, r * BANK : (r + 1) * BANK], summed)
+                    summed = add_route(LAST, r, xc * BANK, BANK, p_of[unit][:, r * BANK : (r + 1) * BANK], [], summed)
                     if r == 0 and xc > 0:
                         project_out(xc - 1)
-            add_waiting()
+            sum_waiting()
             project_out(CHUNKS - 1)

@@ -17,6 +17,7 @@ LAST = BLOCKS - 1
 PAIR = 2
 BLOCK_HEADS = P // HEAD_DIM
 BANK = 512
+SHARED_BANKS = 6
 CHUNKS = TOKENS // BANK
 GROUPS = TOKENS // P
 PAIR_GROUPS = PAIR * GROUPS
@@ -26,7 +27,7 @@ CHUNK_COLS = CHUNK_GROUPS * ROUTES * BLOCK_HEADS
 PARTS = 3
 ROWS = PARTS * CHUNK_COLS
 LIST_COLS = 16
-TENSOR_CHUNKS = 2
+TENSOR_CHUNKS = 3
 
 FLOPS = 2 * DIM * 3 * DIM * TOKENS + 2 * DIM * DIM * TOKENS + 4 * DIM * ROUTES * TOKENS
 
@@ -116,10 +117,11 @@ def tile_cantorattention_b_kernel(tc, x, wqkv, bq, bv, wout, bout, offs, out):
 
         weights_of = {"key": w_key, "q": w_q, "val": w_val}
         bias_of = {"key": None, "q": bias_q, "val": bias_v}
+        table_bufs = {"key": 2, "q": 2, "val": BLOCKS}
         scores = psum.tile([P, BLOCKS * GROUPS, ROUTES, BLOCK_HEADS], F32, name="scores", bufs=1)
 
         def project_sums(name, b, xc):
-            acc = psum.tile([P, BANK], F32, name="acc", bufs=BLOCKS)
+            acc = psum.tile([P, BANK], F32, name="bank", bufs=SHARED_BANKS)
             for kb in range(BLOCKS):
                 nc.tensor.matmul(
                     acc[:],
@@ -132,7 +134,7 @@ def tile_cantorattention_b_kernel(tc, x, wqkv, bq, bv, wout, bout, offs, out):
 
         def store_sums(name, b, xc, acc):
             if xc == 0:
-                table[name, b] = tables.tile([P, TOKENS], F32, name=name)
+                table[name, b] = tables.tile([P, TOKENS], F32, name=name, bufs=table_bufs[name])
             columns = table[name, b][:, xc * BANK : (xc + 1) * BANK]
             if bias_of[name] is None:
                 nc.scalar.copy(columns, acc[:])
@@ -198,7 +200,7 @@ def tile_cantorattention_b_kernel(tc, x, wqkv, bq, bv, wout, bout, offs, out):
                 for i in range(ROUTES):
                     r, xc = (which, i) if b < LAST else (i, which)
                     c = (b % PAIR) * CHUNKS + xc
-                    p_psum = psum.tile([P, BANK], F32, name="p_psum")
+                    p_psum = psum.tile([P, BANK], F32, name="bank", bufs=SHARED_BANKS)
                     for g in range(CHUNK_GROUPS):
                         nc.tensor.matmul(
                             p_psum[:, g * P : (g + 1) * P],
@@ -223,7 +225,7 @@ def tile_cantorattention_b_kernel(tc, x, wqkv, bq, bv, wout, bout, offs, out):
                 return longer
 
             def project_out(xc):
-                accs = [psum.tile([P, BANK], F32, name="acc", bufs=BLOCKS) for ob in range(BLOCKS)]
+                accs = [psum.tile([P, BANK], F32, name="bank", bufs=SHARED_BANKS) for ob in range(BLOCKS)]
                 for kb in range(BLOCKS):
                     for ob in range(BLOCKS):
                         nc.tensor.matmul(
@@ -255,7 +257,7 @@ def tile_cantorattention_b_kernel(tc, x, wqkv, bq, bv, wout, bout, offs, out):
 
             previous = None
             for b in range(BLOCKS):
-                ahead = [("key", b + 1), ("q", b + 1)] if b < LAST else [("val", 0)]
+                ahead = [("key", b + 1), ("q", b + 1), ("val", b)] if b < LAST else [("val", b)]
                 for r in range(ROUTES):
                     prod = ring.tile([P, TOKENS], F32, name="prod")
                     gather_times(prod[:], table["key", b], r, 0, TOKENS, table["q", b][:])
@@ -272,12 +274,11 @@ def tile_cantorattention_b_kernel(tc, x, wqkv, bq, bv, wout, bout, offs, out):
             sum_heads(*previous)
 
             for b in range(LAST):
-                accs = [psum.tile([P, BANK], F32, name="acc", bufs=BLOCKS) for xc in range(TENSOR_CHUNKS)]
+                accs = [psum.tile([P, BANK], F32, name="bank", bufs=SHARED_BANKS) for xc in range(TENSOR_CHUNKS)]
                 summed = None
                 for r in range(ROUTES):
                     unit = b * ROUTES + r
                     summed = add_route(b, r, 0, TOKENS, p_of[unit][:], accs, summed)
-                    store_sums("val", b + 1, r, project_sums("val", b + 1, r))
                     if b < PAIR:
                         softmax_step(1, unit - 1)
                     make_p(unit + 2)

@@ -27,6 +27,7 @@ CHUNK_COLS = CHUNK_GROUPS * ROUTES * BLOCK_HEADS
 PARTS = 3
 ROWS = PARTS * CHUNK_COLS
 LIST_COLS = 16
+FIRST_COLUMN = {"q": 0, "key": DIM, "val": 2 * DIM}
 TENSOR_CHUNKS = 3
 
 FLOPS = 2 * DIM * 3 * DIM * TOKENS + 2 * DIM * DIM * TOKENS + 4 * DIM * ROUTES * TOKENS
@@ -42,7 +43,6 @@ def tile_cantorattention_b_kernel(tc, x, wqkv, bq, bv, wout, bout, offs, out):
         tc.psum_pool(name="psum", bufs=2) as psum,
     ):
         offsets = held.tile([P, ROUTES * TOKENS // LIST_COLS], U16, name="offsets")
-        nc.sync.dma_start(offsets[:], offs)
 
         def route_offsets(r, first, count):
             column = (r * TOKENS + first) // LIST_COLS
@@ -55,9 +55,15 @@ def tile_cantorattention_b_kernel(tc, x, wqkv, bq, bv, wout, bout, offs, out):
             sum_waiting()
 
         def load_weights(queue, name, columns):
-            w = held.tile([P, BLOCKS, DIM], BF16, name=name)
+            w = held.tile([P, BLOCKS, columns.shape[1]], BF16, name=name)
             queue.dma_start(w[:], columns.rearrange("(kb p) c -> p kb c", p=P))
             return w
+
+        weights_of = {}
+
+        def load_block_weights(queue, name, b):
+            first = FIRST_COLUMN[name] + b * P
+            weights_of[name, b] = load_weights(queue, f"w_{name}{b}", wqkv[:, first : first + P])
 
         def load_bias(name, vector):
             bias = held.tile([P, BLOCKS], F32, name=name)
@@ -85,9 +91,11 @@ def tile_cantorattention_b_kernel(tc, x, wqkv, bq, bv, wout, bout, offs, out):
             stacked[:].unsqueeze(2).to_broadcast([ROWS, CHUNK_COLS, HEAD_DIM]),
         )
 
-        w_key = load_weights(nc.sync, "w_key", wqkv[:, DIM : 2 * DIM])
-        w_q = load_weights(nc.scalar, "w_q", wqkv[:, 0:DIM])
+        load_block_weights(nc.sync, "key", 0)
+        load_block_weights(nc.scalar, "q", 0)
         bias_q = load_bias("bias_q", bq)
+        bias_v = load_bias("bias_v", bv)
+        bias_out = load_bias("bias_out", bout)
         x_bf = [held.tile([P, BLOCKS, BANK], BF16, name=f"x_bf{xc}") for xc in range(CHUNKS)]
         with tc.tile_pool(name="stage", bufs=1) as stage:
             for xc in range(CHUNKS):
@@ -95,10 +103,13 @@ def tile_cantorattention_b_kernel(tc, x, wqkv, bq, bv, wout, bout, offs, out):
                 nc.sync.dma_start(x_f32[:], x[:, xc * BANK : (xc + 1) * BANK].rearrange("(kb p) t -> p kb t", p=P))
                 for kb in range(BLOCKS):
                     nc.vector.tensor_copy(x_bf[xc][:, kb, :], x_f32[:, kb, :])
-        w_val = load_weights(nc.sync, "w_val", wqkv[:, 2 * DIM : 3 * DIM])
-        bias_v = load_bias("bias_v", bv)
+        nc.sync.dma_start(offsets[:], offs)
+        for b in range(BLOCKS):
+            load_block_weights(nc.sync, "val", b)
+            if b < LAST:
+                load_block_weights(nc.sync, "key", b + 1)
+                load_block_weights(nc.sync, "q", b + 1)
         w_out = load_weights(nc.sync, "w_out", wout)
-        bias_out = load_bias("bias_out", bout)
 
         table, top, exps, prob, parts, rest, p_rows, p_of = {}, {}, {}, {}, {}, {}, {}, {}
         att = [held.tile([P, TOKENS], BF16, name=f"att{b}") for b in range(BLOCKS)]
@@ -115,7 +126,6 @@ def tile_cantorattention_b_kernel(tc, x, wqkv, bq, bv, wout, bout, offs, out):
             if r > 0:
                 nc.vector.tensor_tensor(longer, summed, weighted[:, len(accs) * BANK :], ALU.add)
 
-        weights_of = {"key": w_key, "q": w_q, "val": w_val}
         bias_of = {"key": None, "q": bias_q, "val": bias_v}
         table_bufs = {"key": 2, "q": 2, "val": BLOCKS}
         scores = psum.tile([P, BLOCKS * GROUPS, ROUTES, BLOCK_HEADS], F32, name="scores", bufs=1)
@@ -125,7 +135,7 @@ def tile_cantorattention_b_kernel(tc, x, wqkv, bq, bv, wout, bout, offs, out):
             for kb in range(BLOCKS):
                 nc.tensor.matmul(
                     acc[:],
-                    lhsT=weights_of[name][:, kb, b * P : (b + 1) * P],
+                    lhsT=weights_of[name, b][:, kb, :],
                     rhs=x_bf[xc][:, kb, :],
                     start=(kb == 0),
                     stop=(kb == BLOCKS - 1),

@@ -38,7 +38,7 @@ def tile_cantorattention_b_kernel(tc, x, wqkv, bq, bv, wout, bout, offs, out):
     with (
         tc.tile_pool(name="held", bufs=1) as held,
         tc.tile_pool(name="tables", bufs=2) as tables,
-        tc.tile_pool(name="soft", bufs=2) as soft,
+        tc.tile_pool(name="soft", bufs=1) as soft,
         tc.tile_pool(name="ring", bufs=3) as ring,
         tc.psum_pool(name="psum", bufs=2) as psum,
     ):
@@ -267,7 +267,11 @@ def tile_cantorattention_b_kernel(tc, x, wqkv, bq, bv, wout, bout, offs, out):
 
             previous = None
             for b in range(BLOCKS):
-                ahead = [("key", b + 1), ("q", b + 1), ("val", b)] if b < LAST else [("val", b)]
+                ahead = [("key", b + 1), ("q", b + 1)] if b < LAST else []
+                if b < PAIR:
+                    ahead.append(("val", b))
+                elif b > PAIR:
+                    ahead.append(("val", b - 1))
                 for r in range(ROUTES):
                     prod = ring.tile([P, TOKENS], F32, name="prod")
                     gather_times(prod[:], table["key", b], r, 0, TOKENS, table["q", b][:])
@@ -284,11 +288,14 @@ def tile_cantorattention_b_kernel(tc, x, wqkv, bq, bv, wout, bout, offs, out):
             sum_heads(*previous)
 
             for b in range(LAST):
-                accs = [psum.tile([P, BANK], F32, name="bank", bufs=SHARED_BANKS) for xc in range(TENSOR_CHUNKS)]
+                tensor_chunks = TENSOR_CHUNKS - 1 if b == 0 else TENSOR_CHUNKS
+                accs = [psum.tile([P, BANK], F32, name="bank", bufs=SHARED_BANKS) for xc in range(tensor_chunks)]
                 summed = None
                 for r in range(ROUTES):
                     unit = b * ROUTES + r
                     summed = add_route(b, r, 0, TOKENS, p_of[unit][:], accs, summed)
+                    if b == 0:
+                        store_sums("val", LAST, r, project_sums("val", LAST, r))
                     if b < PAIR:
                         softmax_step(1, unit - 1)
                     make_p(unit + 2)

@@ -17,7 +17,7 @@ LAST = BLOCKS - 1
 PAIR = 2
 BLOCK_HEADS = P // HEAD_DIM
 BANK = 512
-SHARED_BANKS = 6
+SHARED_BANKS = 7
 CHUNKS = TOKENS // BANK
 GROUPS = TOKENS // P
 PAIR_GROUPS = PAIR * GROUPS
@@ -192,7 +192,7 @@ def tile_cantorattention_b_kernel(tc, x, wqkv, bq, bv, wout, bout, offs, out):
             elif step == 4:
                 nc.vector.tensor_tensor(parts[pair][:, :, 2, :], by_chunk(rest[pair]), parts[pair][:, :, 1, :], ALU.subtract)
             elif step == 5:
-                rows_psum = psum.tile([ROWS, PAIR_CHUNKS * P], BF16, name="rows_psum", bufs=1)
+                rows_psum = psum.tile([ROWS, PAIR_CHUNKS * P], BF16, name="bank", bufs=SHARED_BANKS)
                 for c in range(PAIR_CHUNKS):
                     nc.tensor.transpose(
                         rows_psum[:, c * P : (c + 1) * P], parts[pair][:, c, :, :].rearrange("p k c -> p (k c)"), identity[:]

@@ -65,10 +65,10 @@ def tile_cantorattention_b_kernel(tc, x, wqkv, bq, bv, wout, bout, offs, out):
             first = FIRST_COLUMN[name] + b * P
             weights_of[name, b] = load_weights(queue, f"w_{name}{b}", wqkv[:, first : first + P])
 
-        def load_bias(name, vector):
+        def load_bias(queue, name, vector):
             bias = held.tile([P, BLOCKS], F32, name=name)
             with nc.allow_non_contiguous_dma(reason="one bias element to a partition"):
-                nc.scalar.dma_start(bias[:], vector.rearrange("(b p) o -> p (b o)", p=P))
+                queue.dma_start(bias[:], vector.rearrange("(b p) o -> p (b o)", p=P))
             return bias
 
         identity = held.tile([P, P], BF16, name="identity")
@@ -93,9 +93,7 @@ def tile_cantorattention_b_kernel(tc, x, wqkv, bq, bv, wout, bout, offs, out):
 
         load_block_weights(nc.sync, "key", 0)
         load_block_weights(nc.scalar, "q", 0)
-        bias_q = load_bias("bias_q", bq)
-        bias_v = load_bias("bias_v", bv)
-        bias_out = load_bias("bias_out", bout)
+        bias_q = load_bias(nc.scalar, "bias_q", bq)
         x_bf = [held.tile([P, BLOCKS, BANK], BF16, name=f"x_bf{xc}") for xc in range(CHUNKS)]
         with tc.tile_pool(name="stage", bufs=1) as stage:
             for xc in range(CHUNKS):
@@ -104,12 +102,14 @@ def tile_cantorattention_b_kernel(tc, x, wqkv, bq, bv, wout, bout, offs, out):
                 for kb in range(BLOCKS):
                     nc.vector.tensor_copy(x_bf[xc][:, kb, :], x_f32[:, kb, :])
         nc.sync.dma_start(offsets[:], offs)
+        bias_v = load_bias(nc.sync, "bias_v", bv)
         for b in range(BLOCKS):
             load_block_weights(nc.sync, "val", b)
             if b < LAST:
                 load_block_weights(nc.sync, "key", b + 1)
                 load_block_weights(nc.sync, "q", b + 1)
         w_out = load_weights(nc.sync, "w_out", wout)
+        bias_out = load_bias(nc.sync, "bias_out", bout)
 
         table, top, exps, prob, parts, rest, p_rows, p_of = {}, {}, {}, {}, {}, {}, {}, {}
         att = [held.tile([P, TOKENS], BF16, name=f"att{b}") for b in range(BLOCKS)]

@@ -234,24 +234,24 @@ def tile_cantorattention_b_kernel(tc, x, wqkv, bq, bv, wout, bout, offs, out):
                 waiting["sum"] = (b, r, first, weighted, accs, summed, longer)
                 return longer
 
-            def project_out(xc):
+            def project_out(first, count):
                 accs = [psum.tile([P, BANK], F32, name="bank", bufs=SHARED_BANKS) for ob in range(BLOCKS)]
                 for kb in range(BLOCKS):
                     for ob in range(BLOCKS):
                         nc.tensor.matmul(
-                            accs[ob][:],
+                            accs[ob][:, 0:count],
                             lhsT=w_out[:, kb, ob * P : (ob + 1) * P],
-                            rhs=att[kb][:, xc * BANK : (xc + 1) * BANK],
+                            rhs=att[kb][:, first : first + count],
                             start=(kb == 0),
                             stop=(kb == BLOCKS - 1),
                         )
                 for ob in range(BLOCKS):
-                    result = late.tile([P, BANK], F32, name="result", bufs=BLOCKS)
-                    if xc == CHUNKS - 1 and ob % 2 == 1:
-                        nc.vector.tensor_scalar_add(result[:], accs[ob][:], bias_out[:, ob : ob + 1])
+                    result = late.tile([P, count], F32, name="result", bufs=BLOCKS)
+                    if first + count == TOKENS and ob % 2 == 1:
+                        nc.vector.tensor_scalar_add(result[:], accs[ob][:, 0:count], bias_out[:, ob : ob + 1])
                     else:
-                        nc.scalar.activation(result[:], accs[ob][:], ACT.Identity, bias=bias_out[:, ob : ob + 1])
-                    nc.sync.dma_start(out[ob * P : (ob + 1) * P, xc * BANK : (xc + 1) * BANK], result[:])
+                        nc.scalar.activation(result[:], accs[ob][:, 0:count], ACT.Identity, bias=bias_out[:, ob : ob + 1])
+                    nc.sync.dma_start(out[ob * P : (ob + 1) * P, first : first + count], result[:])
 
             def sum_heads(b, r, prod):
                 prod_bf = ring.tile([P, TOKENS], BF16, name="prod_bf")
@@ -300,13 +300,20 @@ def tile_cantorattention_b_kernel(tc, x, wqkv, bq, bv, wout, bout, offs, out):
                         softmax_step(1, unit - 1)
                     make_p(unit + 2)
 
-            for xc in range(CHUNKS):
+            halves = [(TOKENS - BANK, BANK // 2), (TOKENS - BANK // 2, BANK // 2)]
+            pieces = [(xc * BANK, BANK) for xc in range(CHUNKS - 1)] + halves
+            summed_piece = None
+            for first, count in pieces:
+                xc, inside = divmod(first, BANK)
                 unit = LAST * ROUTES + xc
-                make_p(unit + 2)
+                if inside == 0:
+                    make_p(unit + 2)
                 summed = None
                 for r in range(ROUTES):
-                    summed = add_route(LAST, r, xc * BANK, BANK, p_of[unit][:, r * BANK : (r + 1) * BANK], [], summed)
-                    if r == 0 and xc > 0:
-                        project_out(xc - 1)
+                    p_first = r * BANK + inside
+                    summed = add_route(LAST, r, first, count, p_of[unit][:, p_first : p_first + count], [], summed)
+                    if r == 0 and summed_piece is not None:
+                        project_out(*summed_piece)
+                summed_piece = (first, count)
             sum_waiting()
-            project_out(CHUNKS - 1)
+            project_out(*summed_piece)

@@ -20,15 +20,11 @@ BANK = 512
 SHARED_BANKS = 7
 CHUNKS = TOKENS // BANK
 GROUPS = TOKENS // P
-PAIR_GROUPS = PAIR * GROUPS
-PAIR_CHUNKS = PAIR * CHUNKS
-CHUNK_GROUPS = BANK // P
-CHUNK_COLS = CHUNK_GROUPS * ROUTES * BLOCK_HEADS
-PARTS = 3
-ROWS = PARTS * CHUNK_COLS
+HEAD_GROUPS = BLOCK_HEADS * GROUPS
+BLOCK_ROWS = ROUTES * BLOCK_HEADS
+P_AHEAD = 4
 LIST_COLS = 16
 FIRST_COLUMN = {"q": 0, "key": DIM, "val": 2 * DIM}
-TENSOR_CHUNKS = 3
 
 FLOPS = 2 * DIM * 3 * DIM * TOKENS + 2 * DIM * DIM * TOKENS + 4 * DIM * ROUTES * TOKENS
 
@@ -71,25 +67,12 @@ def tile_cantorattention_b_kernel(tc, x, wqkv, bq, bv, wout, bout, offs, out):
                 queue.dma_start(bias[:], vector.rearrange("(b p) o -> p (b o)", p=P))
             return bias
 
-        identity = held.tile([P, P], BF16, name="identity")
-        masks.make_identity(nc, identity[:])
         identity_f32 = held.tile([P, P], F32, name="identity_f32")
         masks.make_identity(nc, identity_f32[:])
         head_of = held.tile([P, BLOCK_HEADS], BF16, name="head_of")
         nc.vector.memset(head_of[:], 0.0)
         for h in range(BLOCK_HEADS):
             nc.vector.memset(head_of[h * HEAD_DIM : (h + 1) * HEAD_DIM, h : h + 1], 1.0)
-        stacked_two = held.tile([ROWS, CHUNK_COLS], BF16, name="stacked_two")
-        stacked = held.tile([ROWS, CHUNK_COLS], BF16, name="stacked")
-        spread = held.tile([ROWS, CHUNK_GROUPS, ROUTES, P], BF16, name="spread")
-        nc.vector.tensor_tensor(
-            stacked_two[:], identity[0:ROWS, 0:CHUNK_COLS], identity[0:ROWS, CHUNK_COLS : 2 * CHUNK_COLS], ALU.add
-        )
-        nc.vector.tensor_tensor(stacked[:], stacked_two[:], identity[0:ROWS, 2 * CHUNK_COLS : 3 * CHUNK_COLS], ALU.add)
-        nc.vector.tensor_copy(
-            spread[:].rearrange("k g r (h c) -> k (g r h) c", c=HEAD_DIM),
-            stacked[:].unsqueeze(2).to_broadcast([ROWS, CHUNK_COLS, HEAD_DIM]),
-        )
 
         load_block_weights(nc.sync, "key", 0)
         load_block_weights(nc.scalar, "q", 0)
@@ -111,8 +94,9 @@ def tile_cantorattention_b_kernel(tc, x, wqkv, bq, bv, wout, bout, offs, out):
         w_out = load_weights(nc.sync, "w_out", wout)
         bias_out = load_bias(nc.sync, "bias_out", bout)
 
-        table, top, exps, prob, parts, rest, p_rows, p_of = {}, {}, {}, {}, {}, {}, {}, {}
+        table, top, exps, p_of = {}, {}, {}, {}
         att = [held.tile([P, TOKENS], BF16, name=f"att{b}") for b in range(BLOCKS)]
+
         def sum_waiting():
             if waiting["sum"] is None:
                 return
@@ -123,12 +107,12 @@ def tile_cantorattention_b_kernel(tc, x, wqkv, bq, bv, wout, bout, offs, out):
                 nc.tensor.matmul(acc[:], lhsT=identity_f32[:], rhs=weighted[:, columns], start=(r == 0), stop=(r == ROUTES - 1))
                 if r == ROUTES - 1:
                     nc.scalar.copy(att[b][:, first + xc * BANK : first + (xc + 1) * BANK], acc[:])
-            if r > 0:
+            if r > 0 and longer is not None:
                 nc.vector.tensor_tensor(longer, summed, weighted[:, len(accs) * BANK :], ALU.add)
 
         bias_of = {"key": None, "q": bias_q, "val": bias_v}
         table_bufs = {"key": 2, "q": 2, "val": BLOCKS}
-        scores = psum.tile([P, BLOCKS * GROUPS, ROUTES, BLOCK_HEADS], F32, name="scores", bufs=1)
+        scores = psum.tile([P, BLOCKS, ROUTES, BLOCK_HEADS, GROUPS], F32, name="scores", bufs=1)
 
         def project_sums(name, b, xc):
             acc = psum.tile([P, BANK], F32, name="bank", bufs=SHARED_BANKS)
@@ -152,22 +136,22 @@ def tile_cantorattention_b_kernel(tc, x, wqkv, bq, bv, wout, bout, offs, out):
                 nc.scalar.activation(columns, acc[:], ACT.Identity, bias=bias_of[name][:, b : b + 1])
 
         def small_tile(name):
-            return soft.tile([P, PAIR_GROUPS, BLOCK_HEADS], F32, name=name)
+            return soft.tile([P, PAIR, HEAD_GROUPS], F32, name=name)
 
         def full_tile(name):
-            return soft.tile([P, PAIR_GROUPS, ROUTES, BLOCK_HEADS], F32, name=name)
+            return soft.tile([P, PAIR, ROUTES, HEAD_GROUPS], F32, name=name)
 
         def routes_last(columns):
-            return columns.rearrange("p g r h -> p g h r")
+            return columns.rearrange("p b r k -> p b k r")
 
         def over_routes(small):
-            return small[:].unsqueeze(2).to_broadcast([P, PAIR_GROUPS, ROUTES, BLOCK_HEADS])
+            return small[:].unsqueeze(2).to_broadcast([P, PAIR, ROUTES, HEAD_GROUPS])
 
-        def by_chunk(columns):
-            return columns[:].rearrange("p (c g) r h -> p c (g r h)", c=PAIR_CHUNKS)
+        def parked_rows(b):
+            return out[b * BLOCK_ROWS : (b + 1) * BLOCK_ROWS, :]
 
         def softmax_step(pair, step):
-            pair_scores = scores[:, pair * PAIR_GROUPS : (pair + 1) * PAIR_GROUPS, :, :]
+            pair_scores = scores[:, pair * PAIR : (pair + 1) * PAIR, :, :, :].rearrange("p b r h g -> p b r (h g)")
             if step == 0:
                 top[pair] = small_tile("top")
                 nc.vector.tensor_reduce(out=top[pair][:], in_=routes_last(pair_scores), axis=AXIS.X, op=ALU.max)
@@ -181,51 +165,46 @@ def tile_cantorattention_b_kernel(tc, x, wqkv, bq, bv, wout, bout, offs, out):
                 nc.vector.tensor_reduce(out=total[:], in_=routes_last(exps[pair][:]), axis=AXIS.X, op=ALU.add)
                 inverse = small_tile("inverse")
                 nc.vector.reciprocal(inverse[:], total[:])
-                prob[pair] = full_tile("prob")
-                nc.vector.tensor_tensor(prob[pair][:], exps[pair][:], over_routes(inverse), ALU.mult)
-                parts[pair] = soft.tile([P, PAIR_CHUNKS, PARTS, CHUNK_COLS], BF16, name="parts")
-                nc.scalar.copy(parts[pair][:, :, 0, :], by_chunk(prob[pair]))
-            elif step == 3:
-                rest[pair] = full_tile("rest")
-                nc.vector.tensor_tensor(by_chunk(rest[pair]), by_chunk(prob[pair]), parts[pair][:, :, 0, :], ALU.subtract)
-                nc.scalar.copy(parts[pair][:, :, 1, :], by_chunk(rest[pair]))
-            elif step == 4:
-                nc.vector.tensor_tensor(parts[pair][:, :, 2, :], by_chunk(rest[pair]), parts[pair][:, :, 1, :], ALU.subtract)
-            elif step == 5:
-                rows_psum = psum.tile([ROWS, PAIR_CHUNKS * P], BF16, name="bank", bufs=SHARED_BANKS)
-                for c in range(PAIR_CHUNKS):
+                prob = full_tile("prob")
+                nc.vector.tensor_tensor(prob[:], exps[pair][:], over_routes(inverse), ALU.mult)
+                rows_psum = psum.tile([P, PAIR * P], F32, name="bank", bufs=SHARED_BANKS)
+                for j in range(PAIR):
                     nc.tensor.transpose(
-                        rows_psum[:, c * P : (c + 1) * P], parts[pair][:, c, :, :].rearrange("p k c -> p (k c)"), identity[:]
+                        rows_psum[:, j * P : (j + 1) * P], prob[:, j, :, :].rearrange("p r k -> p (r k)"), identity_f32[:]
                     )
-                p_rows[pair] = soft.tile([ROWS, PAIR_CHUNKS * P], BF16, name="p_rows")
-                nc.scalar.copy(p_rows[pair][:], rows_psum[:])
+                p_rows = soft.tile([P, PAIR * P], F32, name="p_rows")
+                nc.scalar.copy(p_rows[:], rows_psum[:])
+                for j in range(PAIR):
+                    nc.sync.dma_start(
+                        parked_rows(pair * PAIR + j).rearrange("q (g i) -> (q g) i", i=P), p_rows[:, j * P : (j + 1) * P]
+                    )
 
         with tc.tile_pool(name="late", bufs=2) as late:
 
-            def make_p(unit):
+            def load_p(unit):
                 if not 0 <= unit < BLOCKS * ROUTES:
                     return
                 b, which = divmod(unit, ROUTES)
-                p_of[unit] = late.tile([P, TOKENS], F32, name="p_block", bufs=4)
-                for i in range(ROUTES):
-                    r, xc = (which, i) if b < LAST else (i, which)
-                    c = (b % PAIR) * CHUNKS + xc
-                    p_psum = psum.tile([P, BANK], F32, name="bank", bufs=SHARED_BANKS)
-                    for g in range(CHUNK_GROUPS):
-                        nc.tensor.matmul(
-                            p_psum[:, g * P : (g + 1) * P],
-                            lhsT=spread[:, g, r, :],
-                            rhs=p_rows[b // PAIR][:, c * P : (c + 1) * P],
-                            start=True,
-                            stop=True,
+                p_of[unit] = late.tile([P, TOKENS], F32, name="p_block", bufs=P_AHEAD)
+                by_head = parked_rows(b).rearrange("(r h) t -> h r t", h=BLOCK_HEADS)
+                for h in range(BLOCK_HEADS):
+                    channels = p_of[unit][h * HEAD_DIM : (h + 1) * HEAD_DIM, :]
+                    if b < LAST:
+                        rows = by_head[h : h + 1, which, :]
+                        nc.sync.dma_start(channels, rows.to_broadcast([HEAD_DIM, TOKENS]))
+                    else:
+                        rows = by_head[h : h + 1, :, which * BANK : (which + 1) * BANK]
+                        nc.sync.dma_start(
+                            channels.rearrange("c (r t) -> c r t", r=ROUTES), rows.to_broadcast([HEAD_DIM, ROUTES, BANK])
                         )
-                    nc.scalar.copy(p_of[unit][:, i * BANK : (i + 1) * BANK], p_psum[:])
 
             def add_route(b, r, first, count, p_columns, accs, summed):
                 weighted = late.tile([P, count], F32, name="weighted", bufs=3)
                 gather_times(weighted[:], table["val", b], r, first, count, p_columns)
                 own = len(accs) * BANK
-                if r == 0:
+                if own == count:
+                    longer = None
+                elif r == 0:
                     longer = weighted[:, own:]
                 elif r < ROUTES - 1:
                     longer = late.tile([P, count - own], F32, name="longer")[:]
@@ -258,47 +237,44 @@ def tile_cantorattention_b_kernel(tc, x, wqkv, bq, bv, wout, bout, offs, out):
                 nc.scalar.copy(prod_bf[:], prod[:])
                 for g in range(GROUPS):
                     nc.tensor.matmul(
-                        scores[:, b * GROUPS + g, r, :], lhsT=prod_bf[:, g * P : (g + 1) * P], rhs=head_of[:], start=True, stop=True
+                        scores[:, b, r, :, g], lhsT=prod_bf[:, g * P : (g + 1) * P], rhs=head_of[:], start=True, stop=True
                     )
 
             for xc in range(CHUNKS):
                 for name in ("key", "q"):
                     store_sums(name, 0, xc, project_sums(name, 0, xc))
 
+            ahead_of = [
+                [("key", 1), ("q", 1), ("val", 0)],
+                [("key", 2), ("q", 2), ("val", 1)],
+                [("key", 3), ("q", 3)],
+                [("val", 2), ("val", 3)],
+            ]
             previous = None
             for b in range(BLOCKS):
-                ahead = [("key", b + 1), ("q", b + 1)] if b < LAST else []
-                if b < PAIR:
-                    ahead.append(("val", b))
-                elif b > PAIR:
-                    ahead.append(("val", b - 1))
                 for r in range(ROUTES):
                     prod = ring.tile([P, TOKENS], F32, name="prod")
                     gather_times(prod[:], table["key", b], r, 0, TOKENS, table["q", b][:])
-                    accs = [project_sums(name, block, r) for name, block in ahead]
+                    accs = [project_sums(name, block, r) for name, block in ahead_of[b]]
                     if previous is not None:
                         sum_heads(*previous)
-                    for (name, block), acc in zip(ahead, accs):
+                    for (name, block), acc in zip(ahead_of[b], accs):
                         store_sums(name, block, r, acc)
-                    if b >= PAIR:
-                        softmax_step(0, (b - PAIR) * ROUTES + r - 1)
+                    if b == PAIR:
+                        softmax_step(0, r - 1)
                     if b == LAST:
-                        make_p(r - 2)
+                        load_p(r)
                     previous = (b, r, prod)
             sum_heads(*previous)
 
             for b in range(LAST):
-                tensor_chunks = TENSOR_CHUNKS - 1 if b == 0 else TENSOR_CHUNKS
-                accs = [psum.tile([P, BANK], F32, name="bank", bufs=SHARED_BANKS) for xc in range(tensor_chunks)]
-                summed = None
+                accs = [psum.tile([P, BANK], F32, name="bank", bufs=SHARED_BANKS) for xc in range(CHUNKS)]
                 for r in range(ROUTES):
                     unit = b * ROUTES + r
-                    summed = add_route(b, r, 0, TOKENS, p_of[unit][:], accs, summed)
+                    add_route(b, r, 0, TOKENS, p_of[unit][:], accs, None)
                     if b == 0:
-                        store_sums("val", LAST, r, project_sums("val", LAST, r))
-                    if b < PAIR:
-                        softmax_step(1, unit - 1)
-                    make_p(unit + 2)
+                        softmax_step(1, r - 1)
+                    load_p(unit + P_AHEAD)
 
             halves = [(TOKENS - BANK, BANK // 2), (TOKENS - BANK // 2, BANK // 2)]
             pieces = [(xc * BANK, BANK) for xc in range(CHUNKS - 1)] + halves
@@ -306,8 +282,6 @@ def tile_cantorattention_b_kernel(tc, x, wqkv, bq, bv, wout, bout, offs, out):
             for first, count in pieces:
                 xc, inside = divmod(first, BANK)
                 unit = LAST * ROUTES + xc
-                if inside == 0:
-                    make_p(unit + 2)
                 summed = None
                 for r in range(ROUTES):
                     p_first = r * BANK + inside

@@ -199,7 +199,10 @@ def tile_cantorattention_b_kernel(tc, x, wqkv, bq, bv, wout, bout, offs, out):
                         )
 
             def add_route(b, r, first, count, p_columns, accs, summed):
-                weighted = late.tile([P, count], F32, name="weighted", bufs=3)
+                if count == TOKENS:
+                    weighted = late.tile([P, count], F32, name="weighted", bufs=3)
+                else:
+                    weighted = late.tile([P, count], F32, name="weighted_piece", bufs=4)
                 gather_times(weighted[:], table["val", b], r, first, count, p_columns)
                 own = len(accs) * BANK
                 if own == count:
@@ -271,9 +274,13 @@ def tile_cantorattention_b_kernel(tc, x, wqkv, bq, bv, wout, bout, offs, out):
                 accs = [psum.tile([P, BANK], F32, name="bank", bufs=SHARED_BANKS) for xc in range(CHUNKS)]
                 for r in range(ROUTES):
                     unit = b * ROUTES + r
-                    add_route(b, r, 0, TOKENS, p_of[unit][:], accs, None)
-                    if b == 0:
-                        softmax_step(1, r - 1)
+                    if unit == 0:
+                        for xc in range(CHUNKS):
+                            columns = slice(xc * BANK, (xc + 1) * BANK)
+                            add_route(b, r, xc * BANK, BANK, p_of[unit][:, columns], accs[xc : xc + 1], None)
+                    else:
+                        add_route(b, r, 0, TOKENS, p_of[unit][:], accs, None)
+                    softmax_step(1, unit - 2)
                     load_p(unit + P_AHEAD)
 
             halves = [(TOKENS - BANK, BANK // 2), (TOKENS - BANK // 2, BANK // 2)]

@@ -20,6 +20,7 @@ BANK = 512
 SHARED_BANKS = 7
 CHUNKS = TOKENS // BANK
 GROUPS = TOKENS // P
+CHUNK_GROUPS = BANK // P
 HEAD_GROUPS = BLOCK_HEADS * GROUPS
 BLOCK_ROWS = ROUTES * BLOCK_HEADS
 P_AHEAD = 4
@@ -67,6 +68,8 @@ def tile_cantorattention_b_kernel(tc, x, wqkv, bq, bv, wout, bout, offs, out):
                 queue.dma_start(bias[:], vector.rearrange("(b p) o -> p (b o)", p=P))
             return bias
 
+        identity = held.tile([P, P], BF16, name="identity")
+        masks.make_identity(nc, identity[:])
         identity_f32 = held.tile([P, P], F32, name="identity_f32")
         masks.make_identity(nc, identity_f32[:])
         head_of = held.tile([P, BLOCK_HEADS], BF16, name="head_of")
@@ -103,10 +106,22 @@ def tile_cantorattention_b_kernel(tc, x, wqkv, bq, bv, wout, bout, offs, out):
             b, r, first, weighted, accs, summed, longer = waiting["sum"]
             waiting["sum"] = None
             for xc, acc in enumerate(accs):
-                columns = slice(xc * BANK, (xc + 1) * BANK)
-                nc.tensor.matmul(acc[:], lhsT=identity_f32[:], rhs=weighted[:, columns], start=(r == 0), stop=(r == ROUTES - 1))
+                for j in range(CHUNK_GROUPS):
+                    nc.tensor.matmul(
+                        acc[:, j * P : (j + 1) * P],
+                        lhsT=weighted[:, xc * BANK + j * P : xc * BANK + (j + 1) * P],
+                        rhs=identity_f32[:],
+                        is_transpose=True,
+                        start=(r == 0 and j == 0),
+                        stop=(r == ROUTES - 1 and j == CHUNK_GROUPS - 1),
+                    )
                 if r == ROUTES - 1:
-                    nc.scalar.copy(att[b][:, first + xc * BANK : first + (xc + 1) * BANK], acc[:])
+                    turned = ring.tile([P, BANK], BF16, name="turned")
+                    nc.scalar.copy(turned[:], acc[:])
+                    back = psum.tile([P, BANK], BF16, name="bank", bufs=SHARED_BANKS)
+                    for j in range(CHUNK_GROUPS):
+                        nc.tensor.transpose(back[:, j * P : (j + 1) * P], turned[:, j * P : (j + 1) * P], identity[:])
+                    nc.scalar.copy(att[b][:, first + xc * BANK : first + (xc + 1) * BANK], back[:])
             if r > 0 and longer is not None:
                 nc.vector.tensor_tensor(longer, summed, weighted[:, len(accs) * BANK :], ALU.add)
 

@@ -68,6 +68,25 @@ def tile_cantorattention_b_kernel(tc, x, wqkv, bq, bv, wout, bout, offs, out):
                 queue.dma_start(bias[:], vector.rearrange("(b p) o -> p (b o)", p=P))
             return bias
 
+        def head_partitions(tile, h):
+            return tile[h : P : BLOCK_HEADS]
+
+        def load_by_head(name, shape, dtype, rows_of_head):
+            mixed = held.tile(shape, dtype, name=name)
+            with nc.allow_non_contiguous_dma(reason="a head's rows go to every other partition"):
+                for h in range(BLOCK_HEADS):
+                    nc.sync.dma_start(head_partitions(mixed, h), rows_of_head[h])
+            return mixed
+
+        def mix_val_weights(b):
+            straight = weights_of["val", b]
+            mixed = held.tile([P, BLOCKS, P], BF16, name=f"w_val_mixed{b}")
+            nc.scalar.copy(
+                mixed[:].rearrange("p kb (c h) -> p kb c h", h=BLOCK_HEADS),
+                straight[:].rearrange("p kb (h c) -> p kb c h", h=BLOCK_HEADS),
+            )
+            weights_of["val", b] = mixed
+
         identity = held.tile([P, P], BF16, name="identity")
         masks.make_identity(nc, identity[:])
         identity_f32 = held.tile([P, P], F32, name="identity_f32")
@@ -88,13 +107,17 @@ def tile_cantorattention_b_kernel(tc, x, wqkv, bq, bv, wout, bout, offs, out):
                 for kb in range(BLOCKS):
                     nc.vector.tensor_copy(x_bf[xc][:, kb, :], x_f32[:, kb, :])
         nc.sync.dma_start(offsets[:], offs)
-        bias_v = load_bias(nc.sync, "bias_v", bv)
+        for b in range(1, BLOCKS):
+            load_block_weights(nc.sync, "key", b)
+            load_block_weights(nc.sync, "q", b)
+        bias_v = load_by_head(
+            "bias_v", [P, BLOCKS], F32, bv.rearrange("(b h c) o -> h c (b o)", h=BLOCK_HEADS, c=HEAD_DIM)
+        )
         for b in range(BLOCKS):
             load_block_weights(nc.sync, "val", b)
-            if b < LAST:
-                load_block_weights(nc.sync, "key", b + 1)
-                load_block_weights(nc.sync, "q", b + 1)
-        w_out = load_weights(nc.sync, "w_out", wout)
+        w_out = load_by_head(
+            "w_out", [P, BLOCKS, DIM], BF16, wout.rearrange("(kb h c) n -> h c kb n", h=BLOCK_HEADS, c=HEAD_DIM)
+        )
         bias_out = load_bias(nc.sync, "bias_out", bout)
 
         table, top, exps, p_of = {}, {}, {}, {}
@@ -126,7 +149,7 @@ def tile_cantorattention_b_kernel(tc, x, wqkv, bq, bv, wout, bout, offs, out):
                 nc.vector.tensor_tensor(longer, summed, weighted[:, len(accs) * BANK :], ALU.add)
 
         bias_of = {"key": None, "q": bias_q, "val": bias_v}
-        table_bufs = {"key": 2, "q": 2, "val": BLOCKS}
+        table_bufs = {"key": 2, "q": 2, "val": 2}
         scores = psum.tile([P, BLOCKS, ROUTES, BLOCK_HEADS, GROUPS], F32, name="scores", bufs=1)
 
         def project_sums(name, b, xc):
@@ -203,7 +226,7 @@ def tile_cantorattention_b_kernel(tc, x, wqkv, bq, bv, wout, bout, offs, out):
                 p_of[unit] = late.tile([P, TOKENS], F32, name="p_block", bufs=P_AHEAD)
                 by_head = parked_rows(b).rearrange("(r h) t -> h r t", h=BLOCK_HEADS)
                 for h in range(BLOCK_HEADS):
-                    channels = p_of[unit][h * HEAD_DIM : (h + 1) * HEAD_DIM, :]
+                    channels = head_partitions(p_of[unit], h)
                     if b < LAST:
                         rows = by_head[h : h + 1, which, :]
                         nc.sync.dma_start(channels, rows.to_broadcast([HEAD_DIM, TOKENS]))
@@ -262,14 +285,11 @@ def tile_cantorattention_b_kernel(tc, x, wqkv, bq, bv, wout, bout, offs, out):
                 for name in ("key", "q"):
                     store_sums(name, 0, xc, project_sums(name, 0, xc))
 
-            ahead_of = [
-                [("key", 1), ("q", 1), ("val", 0)],
-                [("key", 2), ("q", 2), ("val", 1)],
-                [("key", 3), ("q", 3)],
-                [("val", 2), ("val", 3)],
-            ]
+            ahead_of = [[("key", 1), ("q", 1)], [("key", 2), ("q", 2)], [("key", 3), ("q", 3)], [("val", 0)]]
             previous = None
             for b in range(BLOCKS):
+                if b == LAST:
+                    mix_val_weights(0)
                 for r in range(ROUTES):
                     prod = ring.tile([P, TOKENS], F32, name="prod")
                     gather_times(prod[:], table["key", b], r, 0, TOKENS, table["q", b][:])
@@ -287,6 +307,7 @@ def tile_cantorattention_b_kernel(tc, x, wqkv, bq, bv, wout, bout, offs, out):
 
             for b in range(LAST):
                 accs = [psum.tile([P, BANK], F32, name="bank", bufs=SHARED_BANKS) for xc in range(CHUNKS)]
+                mix_val_weights(b + 1)
                 for r in range(ROUTES):
                     unit = b * ROUTES + r
                     if unit == 0:
@@ -295,6 +316,7 @@ def tile_cantorattention_b_kernel(tc, x, wqkv, bq, bv, wout, bout, offs, out):
                             add_route(b, r, xc * BANK, BANK, p_of[unit][:, columns], accs[xc : xc + 1], None)
                     else:
                         add_route(b, r, 0, TOKENS, p_of[unit][:], accs, None)
+                    store_sums("val", b + 1, r, project_sums("val", b + 1, r))
                     softmax_step(1, unit - 2)
                     load_p(unit + P_AHEAD)
 

@@ -17,12 +17,13 @@ LAST = BLOCKS - 1
 PAIR = 2
 BLOCK_HEADS = P // HEAD_DIM
 BANK = 512
-SHARED_BANKS = 7
+SHARED_BANKS = 8
 CHUNKS = TOKENS // BANK
 GROUPS = TOKENS // P
 CHUNK_GROUPS = BANK // P
 HEAD_GROUPS = BLOCK_HEADS * GROUPS
 BLOCK_ROWS = ROUTES * BLOCK_HEADS
+LAST_TENSOR_CHUNKS = 1
 P_AHEAD = 4
 LIST_COLS = 16
 FIRST_COLUMN = {"q": 0, "key": DIM, "val": 2 * DIM}
@@ -150,7 +151,7 @@ def tile_cantorattention_b_kernel(tc, x, wqkv, bq, bv, wout, bout, offs, out):
 
         bias_of = {"key": None, "q": bias_q, "val": bias_v}
         table_bufs = {"key": 2, "q": 2, "val": 2}
-        scores = psum.tile([P, BLOCKS, ROUTES, BLOCK_HEADS, GROUPS], F32, name="scores", bufs=1)
+        scores = psum.tile([P, BLOCKS, ROUTES, BLOCK_HEADS, GROUPS], F32, name="bank", bufs=SHARED_BANKS)
 
         def project_sums(name, b, xc):
             acc = psum.tile([P, BANK], F32, name="bank", bufs=SHARED_BANKS)
@@ -238,9 +239,9 @@ def tile_cantorattention_b_kernel(tc, x, wqkv, bq, bv, wout, bout, offs, out):
 
             def add_route(b, r, first, count, p_columns, accs, summed):
                 if count == TOKENS:
-                    weighted = late.tile([P, count], F32, name="weighted", bufs=3)
+                    weighted = ring.tile([P, count], F32, name="prod")
                 else:
-                    weighted = late.tile([P, count], F32, name="weighted_piece", bufs=4)
+                    weighted = late.tile([P, count], F32, name="weighted_piece", bufs=2 * ROUTES)
                 gather_times(weighted[:], table["val", b], r, first, count, p_columns)
                 own = len(accs) * BANK
                 if own == count:
@@ -281,9 +282,8 @@ def tile_cantorattention_b_kernel(tc, x, wqkv, bq, bv, wout, bout, offs, out):
                         scores[:, b, r, :, g], lhsT=prod_bf[:, g * P : (g + 1) * P], rhs=head_of[:], start=True, stop=True
                     )
 
-            for xc in range(CHUNKS):
-                for name in ("key", "q"):
-                    store_sums(name, 0, xc, project_sums(name, 0, xc))
+            for name, xc in (("key", 0), ("q", 0), ("key", 1), ("q", 1), ("key", 2), ("key", 3), ("q", 2), ("q", 3)):
+                store_sums(name, 0, xc, project_sums(name, 0, xc))
 
             ahead_of = [[("key", 1), ("q", 1)], [("key", 2), ("q", 2)], [("key", 3), ("q", 3)], [("val", 0)]]
             previous = None
@@ -292,7 +292,10 @@ def tile_cantorattention_b_kernel(tc, x, wqkv, bq, bv, wout, bout, offs, out):
                     mix_val_weights(0)
                 for r in range(ROUTES):
                     prod = ring.tile([P, TOKENS], F32, name="prod")
-                    gather_times(prod[:], table["key", b], r, 0, TOKENS, table["q", b][:])
+                    count = TOKENS // 2 if previous is None else TOKENS
+                    for first in range(0, TOKENS, count):
+                        tokens = slice(first, first + count)
+                        gather_times(prod[:, tokens], table["key", b], r, first, count, table["q", b][:, tokens])
                     accs = [project_sums(name, block, r) for name, block in ahead_of[b]]
                     if previous is not None:
                         sum_heads(*previous)
@@ -326,10 +329,11 @@ def tile_cantorattention_b_kernel(tc, x, wqkv, bq, bv, wout, bout, offs, out):
             for first, count in pieces:
                 xc, inside = divmod(first, BANK)
                 unit = LAST * ROUTES + xc
+                accs = [psum.tile([P, BANK], F32, name="bank", bufs=SHARED_BANKS)] if xc < LAST_TENSOR_CHUNKS else []
                 summed = None
                 for r in range(ROUTES):
                     p_first = r * BANK + inside
-                    summed = add_route(LAST, r, first, count, p_of[unit][:, p_first : p_first + count], [], summed)
+                    summed = add_route(LAST, r, first, count, p_of[unit][:, p_first : p_first + count], accs, summed)
                     if r == 0 and summed_piece is not None:
                         project_out(*summed_piece)
                 summed_piece = (first, count)

@@ -19,6 +19,8 @@ BLOCK_HEADS = P // HEAD_DIM
 BANK = 512
 SHARED_BANKS = 8
 CHUNKS = TOKENS // BANK
+LAST_HALVES = [(TOKENS - BANK, BANK // 2), (TOKENS - BANK // 2, BANK // 2)]
+CHUNKS_LAST_HALVED = [(xc * BANK, BANK) for xc in range(CHUNKS - 1)] + LAST_HALVES
 GROUPS = TOKENS // P
 CHUNK_GROUPS = BANK // P
 HEAD_GROUPS = BLOCK_HEADS * GROUPS
@@ -102,11 +104,12 @@ def tile_cantorattention_b_kernel(tc, x, wqkv, bq, bv, wout, bout, offs, out):
         bias_q = load_bias(nc.scalar, "bias_q", bq)
         x_bf = [held.tile([P, BLOCKS, BANK], BF16, name=f"x_bf{xc}") for xc in range(CHUNKS)]
         with tc.tile_pool(name="stage", bufs=1) as stage:
-            for xc in range(CHUNKS):
-                x_f32 = stage.tile([P, BLOCKS, BANK], F32, name=f"x_f32_{xc}")
-                nc.sync.dma_start(x_f32[:], x[:, xc * BANK : (xc + 1) * BANK].rearrange("(kb p) t -> p kb t", p=P))
+            for first, count in CHUNKS_LAST_HALVED:
+                xc, inside = divmod(first, BANK)
+                x_f32 = stage.tile([P, BLOCKS, count], F32, name=f"x_f32_{first}")
+                nc.sync.dma_start(x_f32[:], x[:, first : first + count].rearrange("(kb p) t -> p kb t", p=P))
                 for kb in range(BLOCKS):
-                    nc.vector.tensor_copy(x_bf[xc][:, kb, :], x_f32[:, kb, :])
+                    nc.vector.tensor_copy(x_bf[xc][:, kb, inside : inside + count], x_f32[:, kb, :])
         nc.sync.dma_start(offsets[:], offs)
         for b in range(1, BLOCKS):
             load_block_weights(nc.sync, "key", b)
@@ -153,26 +156,27 @@ def tile_cantorattention_b_kernel(tc, x, wqkv, bq, bv, wout, bout, offs, out):
         table_bufs = {"key": 2, "q": 2, "val": 2}
         scores = psum.tile([P, BLOCKS, ROUTES, BLOCK_HEADS, GROUPS], F32, name="bank", bufs=SHARED_BANKS)
 
-        def project_sums(name, b, xc):
+        def project_sums(name, b, first, count=BANK):
+            xc, inside = divmod(first, BANK)
             acc = psum.tile([P, BANK], F32, name="bank", bufs=SHARED_BANKS)
             for kb in range(BLOCKS):
                 nc.tensor.matmul(
-                    acc[:],
+                    acc[:, 0:count],
                     lhsT=weights_of[name, b][:, kb, :],
-                    rhs=x_bf[xc][:, kb, :],
+                    rhs=x_bf[xc][:, kb, inside : inside + count],
                     start=(kb == 0),
                     stop=(kb == BLOCKS - 1),
                 )
             return acc
 
-        def store_sums(name, b, xc, acc):
-            if xc == 0:
+        def store_sums(name, b, first, acc, count=BANK):
+            if first == 0:
                 table[name, b] = tables.tile([P, TOKENS], F32, name=name, bufs=table_bufs[name])
-            columns = table[name, b][:, xc * BANK : (xc + 1) * BANK]
+            columns = table[name, b][:, first : first + count]
             if bias_of[name] is None:
-                nc.scalar.copy(columns, acc[:])
+                nc.scalar.copy(columns, acc[:, 0:count])
             else:
-                nc.scalar.activation(columns, acc[:], ACT.Identity, bias=bias_of[name][:, b : b + 1])
+                nc.scalar.activation(columns, acc[:, 0:count], ACT.Identity, bias=bias_of[name][:, b : b + 1])
 
         def small_tile(name):
             return soft.tile([P, PAIR, HEAD_GROUPS], F32, name=name)
@@ -267,7 +271,7 @@ def tile_cantorattention_b_kernel(tc, x, wqkv, bq, bv, wout, bout, offs, out):
                             stop=(kb == BLOCKS - 1),
                         )
                 for ob in range(BLOCKS):
-                    result = late.tile([P, count], F32, name="result", bufs=BLOCKS)
+                    result = late.tile([P, count], F32, name="result", bufs=2 * BLOCKS)
                     if first + count == TOKENS and ob % 2 == 1:
                         nc.vector.tensor_scalar_add(result[:], accs[ob][:, 0:count], bias_out[:, ob : ob + 1])
                     else:
@@ -282,8 +286,13 @@ def tile_cantorattention_b_kernel(tc, x, wqkv, bq, bv, wout, bout, offs, out):
                         scores[:, b, r, :, g], lhsT=prod_bf[:, g * P : (g + 1) * P], rhs=head_of[:], start=True, stop=True
                     )
 
-            for name, xc in (("key", 0), ("q", 0), ("key", 1), ("q", 1), ("key", 2), ("key", 3), ("q", 2), ("q", 3)):
-                store_sums(name, 0, xc, project_sums(name, 0, xc))
+            for xc in range(CHUNKS // 2):
+                for name in ("key", "q"):
+                    store_sums(name, 0, xc * BANK, project_sums(name, 0, xc * BANK))
+            for first, count in CHUNKS_LAST_HALVED[CHUNKS // 2 :]:
+                store_sums("key", 0, first, project_sums("key", 0, first, count), count)
+            for xc in range(CHUNKS // 2, CHUNKS):
+                store_sums("q", 0, xc * BANK, project_sums("q", 0, xc * BANK))
 
             ahead_of = [[("key", 1), ("q", 1)], [("key", 2), ("q", 2)], [("key", 3), ("q", 3)], [("val", 0)]]
             previous = None
@@ -296,11 +305,11 @@ def tile_cantorattention_b_kernel(tc, x, wqkv, bq, bv, wout, bout, offs, out):
                     for first in range(0, TOKENS, count):
                         tokens = slice(first, first + count)
                         gather_times(prod[:, tokens], table["key", b], r, first, count, table["q", b][:, tokens])
-                    accs = [project_sums(name, block, r) for name, block in ahead_of[b]]
+                    accs = [project_sums(name, block, r * BANK) for name, block in ahead_of[b]]
                     if previous is not None:
                         sum_heads(*previous)
                     for (name, block), acc in zip(ahead_of[b], accs):
-                        store_sums(name, block, r, acc)
+                        store_sums(name, block, r * BANK, acc)
                     if b == PAIR:
                         softmax_step(0, r - 1)
                     if b == LAST:
@@ -319,14 +328,12 @@ def tile_cantorattention_b_kernel(tc, x, wqkv, bq, bv, wout, bout, offs, out):
                             add_route(b, r, xc * BANK, BANK, p_of[unit][:, columns], accs[xc : xc + 1], None)
                     else:
                         add_route(b, r, 0, TOKENS, p_of[unit][:], accs, None)
-                    store_sums("val", b + 1, r, project_sums("val", b + 1, r))
+                    store_sums("val", b + 1, r * BANK, project_sums("val", b + 1, r * BANK))
                     softmax_step(1, unit - 2)
                     load_p(unit + P_AHEAD)
 
-            halves = [(TOKENS - BANK, BANK // 2), (TOKENS - BANK // 2, BANK // 2)]
-            pieces = [(xc * BANK, BANK) for xc in range(CHUNKS - 1)] + halves
             summed_piece = None
-            for first, count in pieces:
+            for first, count in CHUNKS_LAST_HALVED:
                 xc, inside = divmod(first, BANK)
                 unit = LAST * ROUTES + xc
                 accs = [psum.tile([P, BANK], F32, name="bank", bufs=SHARED_BANKS)] if xc < LAST_TENSOR_CHUNKS else []

@@ -26,7 +26,7 @@ CHUNK_GROUPS = BANK // P
 HEAD_GROUPS = BLOCK_HEADS * GROUPS
 BLOCK_ROWS = ROUTES * BLOCK_HEADS
 LAST_TENSOR_CHUNKS = 1
-P_AHEAD = 4
+P_AHEAD = 6
 LIST_COLS = 16
 FIRST_COLUMN = {"q": 0, "key": DIM, "val": 2 * DIM}
 
@@ -94,6 +94,14 @@ def tile_cantorattention_b_kernel(tc, x, wqkv, bq, bv, wout, bout, offs, out):
         masks.make_identity(nc, identity[:])
         identity_f32 = held.tile([P, P], F32, name="identity_f32")
         masks.make_identity(nc, identity_f32[:])
+        one_route = held.tile([P, HEAD_GROUPS], F32, name="one_route")
+        nc.vector.tensor_reduce(
+            out=one_route[:], in_=identity_f32[:].rearrange("p (r k) -> p k r", r=ROUTES), axis=AXIS.X, op=ALU.add
+        )
+        same_head_group = held.tile([P, ROUTES, HEAD_GROUPS], F32, name="same_head_group")
+        nc.vector.tensor_copy(same_head_group[:], one_route[:].unsqueeze(1).to_broadcast([P, ROUTES, HEAD_GROUPS]))
+        minus_inverse_scale = held.tile([P, P], F32, name="minus_inverse_scale")
+        nc.vector.tensor_scalar_mul(minus_inverse_scale[:], identity_f32[:], -1.0 / SCALE)
         head_of = held.tile([P, BLOCK_HEADS], BF16, name="head_of")
         nc.vector.memset(head_of[:], 0.0)
         for h in range(BLOCK_HEADS):
@@ -193,6 +201,29 @@ def tile_cantorattention_b_kernel(tc, x, wqkv, bq, bv, wout, bout, offs, out):
         def parked_rows(b):
             return out[b * BLOCK_ROWS : (b + 1) * BLOCK_ROWS, :]
 
+        def rows_bank():
+            return psum.tile([P, PAIR * P], F32, name="bank", bufs=SHARED_BANKS)
+
+        def rows_tile(name):
+            return soft.tile([P, PAIR * P], F32, name=name)
+
+        def turn_to_rows(bank, columns, last):
+            for j in range(PAIR):
+                nc.tensor.matmul(
+                    bank[:, j * P : (j + 1) * P],
+                    lhsT=columns[:, j, :, :].rearrange("p r k -> p (r k)"),
+                    rhs=identity_f32[:],
+                    is_transpose=True,
+                    start=(j == 0),
+                    stop=(last and j == PAIR - 1),
+                )
+
+        def park(pair, p_rows):
+            for j in range(PAIR):
+                nc.sync.dma_start(
+                    parked_rows(pair * PAIR + j).rearrange("q (g i) -> (q g) i", i=P), p_rows[:, j * P : (j + 1) * P]
+                )
+
         def softmax_step(pair, step):
             pair_scores = scores[:, pair * PAIR : (pair + 1) * PAIR, :, :, :].rearrange("p b r h g -> p b r (h g)")
             if step == 0:
@@ -201,26 +232,38 @@ def tile_cantorattention_b_kernel(tc, x, wqkv, bq, bv, wout, bout, offs, out):
             elif step == 1:
                 shifted = full_tile("shifted")
                 nc.vector.tensor_tensor(shifted[:], pair_scores, over_routes(top[pair]), ALU.subtract)
-                exps[pair] = full_tile("exps")
-                nc.scalar.activation(exps[pair][:], shifted[:], ACT.Exp, scale=SCALE)
-            elif step == 2:
+                if pair == 0:
+                    exps[pair] = full_tile("exps")
+                    nc.scalar.activation(exps[pair][:], shifted[:], ACT.Exp, scale=SCALE)
+                else:
+                    shifted_rows = rows_bank()
+                    turn_to_rows(shifted_rows, shifted, True)
+                    exp_rows = rows_tile("exp_rows")
+                    nc.scalar.activation(exp_rows[:], shifted_rows[:], ACT.Exp, scale=SCALE)
+                    sum_rows = rows_bank()
+                    nc.tensor.matmul(
+                        sum_rows[:], lhsT=same_head_group[:].rearrange("p r k -> p (r k)"), rhs=exp_rows[:], start=True, stop=True
+                    )
+                    log_rows = rows_tile("log_rows")
+                    nc.scalar.activation(log_rows[:], sum_rows[:], ACT.Ln)
+                    exponent_rows = rows_bank()
+                    turn_to_rows(exponent_rows, shifted, False)
+                    nc.tensor.matmul(exponent_rows[:], lhsT=minus_inverse_scale[:], rhs=log_rows[:], start=False, stop=True)
+                    p_rows = rows_tile("p_rows")
+                    nc.scalar.activation(p_rows[:], exponent_rows[:], ACT.Exp, scale=SCALE)
+                    park(pair, p_rows)
+            elif step == 2 and pair == 0:
                 total = small_tile("total")
                 nc.vector.tensor_reduce(out=total[:], in_=routes_last(exps[pair][:]), axis=AXIS.X, op=ALU.add)
                 inverse = small_tile("inverse")
                 nc.vector.reciprocal(inverse[:], total[:])
                 prob = full_tile("prob")
                 nc.vector.tensor_tensor(prob[:], exps[pair][:], over_routes(inverse), ALU.mult)
-                rows_psum = psum.tile([P, PAIR * P], F32, name="bank", bufs=SHARED_BANKS)
-                for j in range(PAIR):
-                    nc.tensor.transpose(
-                        rows_psum[:, j * P : (j + 1) * P], prob[:, j, :, :].rearrange("p r k -> p (r k)"), identity_f32[:]
-                    )
-                p_rows = soft.tile([P, PAIR * P], F32, name="p_rows")
-                nc.scalar.copy(p_rows[:], rows_psum[:])
-                for j in range(PAIR):
-                    nc.sync.dma_start(
-                        parked_rows(pair * PAIR + j).rearrange("q (g i) -> (q g) i", i=P), p_rows[:, j * P : (j + 1) * P]
-                    )
+                prob_rows = rows_bank()
+                turn_to_rows(prob_rows, prob, True)
+                p_rows = rows_tile("p_rows")
+                nc.scalar.copy(p_rows[:], prob_rows[:])
+                park(pair, p_rows)
 
         with tc.tile_pool(name="late", bufs=2) as late:
 
@@ -312,8 +355,9 @@ def tile_cantorattention_b_kernel(tc, x, wqkv, bq, bv, wout, bout, offs, out):
                         store_sums(name, block, r * BANK, acc)
                     if b == PAIR:
                         softmax_step(0, r - 1)
-                    if b == LAST:
-                        load_p(r)
+                    if (b, r) == (LAST, 0):
+                        for unit in range(P_AHEAD):
+                            load_p(unit)
                     previous = (b, r, prod)
             sum_heads(*previous)
 
@@ -329,7 +373,7 @@ def tile_cantorattention_b_kernel(tc, x, wqkv, bq, bv, wout, bout, offs, out):
                     else:
                         add_route(b, r, 0, TOKENS, p_of[unit][:], accs, None)
                     store_sums("val", b + 1, r * BANK, project_sums("val", b + 1, r * BANK))
-                    softmax_step(1, unit - 2)
+                    softmax_step(1, unit)
                     load_p(unit + P_AHEAD)
 
             summed_piece = None

@@ -302,17 +302,24 @@ def tile_cantorattention_b_kernel(tc, x, wqkv, bq, bv, wout, bout, offs, out):
                 waiting["sum"] = (b, r, first, weighted, accs, summed, longer)
                 return longer
 
-            def project_out(first, count):
+            def out_terms(accs, kb, first, count):
+                for ob in range(BLOCKS):
+                    nc.tensor.matmul(
+                        accs[ob][:, 0:count],
+                        lhsT=w_out[:, kb, ob * P : (ob + 1) * P],
+                        rhs=att[kb][:, first : first + count],
+                        start=(kb == 0),
+                        stop=(kb == LAST),
+                    )
+
+            def open_out(first, count):
                 accs = [psum.tile([P, BANK], F32, name="bank", bufs=SHARED_BANKS) for ob in range(BLOCKS)]
-                for kb in range(BLOCKS):
-                    for ob in range(BLOCKS):
-                        nc.tensor.matmul(
-                            accs[ob][:, 0:count],
-                            lhsT=w_out[:, kb, ob * P : (ob + 1) * P],
-                            rhs=att[kb][:, first : first + count],
-                            start=(kb == 0),
-                            stop=(kb == BLOCKS - 1),
-                        )
+                for kb in range(LAST):
+                    out_terms(accs, kb, first, count)
+                return accs
+
+            def close_out(first, count, accs):
+                out_terms(accs, LAST, first, count)
                 for ob in range(BLOCKS):
                     result = late.tile([P, count], F32, name="result", bufs=2 * BLOCKS)
                     if first + count == TOKENS and ob % 2 == 1:
@@ -366,12 +373,7 @@ def tile_cantorattention_b_kernel(tc, x, wqkv, bq, bv, wout, bout, offs, out):
                 mix_val_weights(b + 1)
                 for r in range(ROUTES):
                     unit = b * ROUTES + r
-                    if unit == 0:
-                        for xc in range(CHUNKS):
-                            columns = slice(xc * BANK, (xc + 1) * BANK)
-                            add_route(b, r, xc * BANK, BANK, p_of[unit][:, columns], accs[xc : xc + 1], None)
-                    else:
-                        add_route(b, r, 0, TOKENS, p_of[unit][:], accs, None)
+                    add_route(b, r, 0, TOKENS, p_of[unit][:], accs, None)
                     store_sums("val", b + 1, r * BANK, project_sums("val", b + 1, r * BANK))
                     softmax_step(1, unit)
                     load_p(unit + P_AHEAD)
@@ -385,8 +387,10 @@ def tile_cantorattention_b_kernel(tc, x, wqkv, bq, bv, wout, bout, offs, out):
                 for r in range(ROUTES):
                     p_first = r * BANK + inside
                     summed = add_route(LAST, r, first, count, p_of[unit][:, p_first : p_first + count], accs, summed)
-                    if r == 0 and summed_piece is not None:
-                        project_out(*summed_piece)
-                summed_piece = (first, count)
+                    if r == 0:
+                        if summed_piece is not None:
+                            close_out(*summed_piece)
+                        opened = open_out(first, count)
+                summed_piece = (first, count, opened)
             sum_waiting()
-            project_out(*summed_piece)
+            close_out(*summed_piece)

import concourse.masks as masks
import concourse.mybir as mybir

F32, BF16, U16 = mybir.dt.float32, mybir.dt.bfloat16, mybir.dt.uint16
ALU = mybir.AluOpType
ACT = mybir.ActivationFunctionType
AXIS = mybir.AxisListType

P = 128
DIM = 512
TOKENS = 2048
ROUTES = 4
HEAD_DIM = 64
SCALE = 0.125
BLOCKS = DIM // P
LAST = BLOCKS - 1
PAIR = 2
BLOCK_HEADS = P // HEAD_DIM
BANK = 512
SHARED_BANKS = 8
CHUNKS = TOKENS // BANK
LAST_HALVES = [(TOKENS - BANK, BANK // 2), (TOKENS - BANK // 2, BANK // 2)]
CHUNKS_LAST_HALVED = [(xc * BANK, BANK) for xc in range(CHUNKS - 1)] + LAST_HALVES
GROUPS = TOKENS // P
CHUNK_GROUPS = BANK // P
HEAD_GROUPS = BLOCK_HEADS * GROUPS
BLOCK_ROWS = ROUTES * BLOCK_HEADS
LAST_TENSOR_CHUNKS = 1
P_AHEAD = 6
LIST_COLS = 16
FIRST_COLUMN = {"q": 0, "key": DIM, "val": 2 * DIM}

FLOPS = 2 * DIM * 3 * DIM * TOKENS + 2 * DIM * DIM * TOKENS + 4 * DIM * ROUTES * TOKENS


def tile_cantorattention_b_kernel(tc, x, wqkv, bq, bv, wout, bout, offs, out):
    nc = tc.nc
    with (
        tc.tile_pool(name="held", bufs=1) as held,
        tc.tile_pool(name="tables", bufs=2) as tables,
        tc.tile_pool(name="soft", bufs=1) as soft,
        tc.tile_pool(name="ring", bufs=3) as ring,
        tc.psum_pool(name="psum", bufs=2) as psum,
    ):
        offsets = held.tile([P, ROUTES * TOKENS // LIST_COLS], U16, name="offsets")

        def route_offsets(r, first, count):
            column = (r * TOKENS + first) // LIST_COLS
            return offsets[:, column : column + count // LIST_COLS]

        waiting = {"sum": None}

        def gather_times(product, window, r, first, count, other):
            nc.vector.tensor_tensor(product, window[:].indirect(route_offsets(r, first, count)), other, ALU.mult)
            sum_waiting()

        def load_weights(queue, name, columns):
            w = held.tile([P, BLOCKS, columns.shape[1]], BF16, name=name)
            queue.dma_start(w[:], columns.rearrange("(kb p) c -> p kb c", p=P))
            return w

        weights_of = {}

        def load_block_weights(queue, name, b):
            first = FIRST_COLUMN[name] + b * P
            weights_of[name, b] = load_weights(queue, f"w_{name}{b}", wqkv[:, first : first + P])

        def load_bias(queue, name, vector):
            bias = held.tile([P, BLOCKS], F32, name=name)
            with nc.allow_non_contiguous_dma(reason="one bias element to a partition"):
                queue.dma_start(bias[:], vector.rearrange("(b p) o -> p (b o)", p=P))
            return bias

        def head_partitions(tile, h):
            return tile[h : P : BLOCK_HEADS]

        def load_by_head(name, shape, dtype, rows_of_head):
            mixed = held.tile(shape, dtype, name=name)
            with nc.allow_non_contiguous_dma(reason="a head's rows go to every other partition"):
                for h in range(BLOCK_HEADS):
                    nc.sync.dma_start(head_partitions(mixed, h), rows_of_head[h])
            return mixed

        def mix_val_weights(b):
            straight = weights_of["val", b]
            mixed = held.tile([P, BLOCKS, P], BF16, name=f"w_val_mixed{b}")
            nc.scalar.copy(
                mixed[:].rearrange("p kb (c h) -> p kb c h", h=BLOCK_HEADS),
                straight[:].rearrange("p kb (h c) -> p kb c h", h=BLOCK_HEADS),
            )
            weights_of["val", b] = mixed

        identity = held.tile([P, P], BF16, name="identity")
        masks.make_identity(nc, identity[:])
        identity_f32 = held.tile([P, P], F32, name="identity_f32")
        masks.make_identity(nc, identity_f32[:])
        one_route = held.tile([P, HEAD_GROUPS], F32, name="one_route")
        nc.vector.tensor_reduce(
            out=one_route[:], in_=identity_f32[:].rearrange("p (r k) -> p k r", r=ROUTES), axis=AXIS.X, op=ALU.add
        )
        same_head_group = held.tile([P, ROUTES, HEAD_GROUPS], F32, name="same_head_group")
        nc.vector.tensor_copy(same_head_group[:], one_route[:].unsqueeze(1).to_broadcast([P, ROUTES, HEAD_GROUPS]))
        minus_inverse_scale = held.tile([P, P], F32, name="minus_inverse_scale")
        nc.vector.tensor_scalar_mul(minus_inverse_scale[:], identity_f32[:], -1.0 / SCALE)
        head_of = held.tile([P, BLOCK_HEADS], BF16, name="head_of")
        nc.vector.memset(head_of[:], 0.0)
        for h in range(BLOCK_HEADS):
            nc.vector.memset(head_of[h * HEAD_DIM : (h + 1) * HEAD_DIM, h : h + 1], 1.0)

        load_block_weights(nc.sync, "key", 0)
        load_block_weights(nc.scalar, "q", 0)
        bias_q = load_bias(nc.scalar, "bias_q", bq)
        x_bf = [held.tile([P, BLOCKS, BANK], BF16, name=f"x_bf{xc}") for xc in range(CHUNKS)]
        with tc.tile_pool(name="stage", bufs=1) as stage:
            for first, count in CHUNKS_LAST_HALVED:
                xc, inside = divmod(first, BANK)
                x_f32 = stage.tile([P, BLOCKS, count], F32, name=f"x_f32_{first}")
                nc.sync.dma_start(x_f32[:], x[:, first : first + count].rearrange("(kb p) t -> p kb t", p=P))
                for kb in range(BLOCKS):
                    nc.vector.tensor_copy(x_bf[xc][:, kb, inside : inside + count], x_f32[:, kb, :])
        nc.sync.dma_start(offsets[:], offs)
        for b in range(1, BLOCKS):
            load_block_weights(nc.sync, "key", b)
            load_block_weights(nc.sync, "q", b)
        bias_v = load_by_head(
            "bias_v", [P, BLOCKS], F32, bv.rearrange("(b h c) o -> h c (b o)", h=BLOCK_HEADS, c=HEAD_DIM)
        )
        for b in range(BLOCKS):
            load_block_weights(nc.sync, "val", b)
        w_out = load_by_head(
            "w_out", [P, BLOCKS, DIM], BF16, wout.rearrange("(kb h c) n -> h c kb n", h=BLOCK_HEADS, c=HEAD_DIM)
        )
        bias_out = load_bias(nc.sync, "bias_out", bout)

        table, top, exps, p_of = {}, {}, {}, {}
        att = [held.tile([P, TOKENS], BF16, name=f"att{b}") for b in range(BLOCKS)]

        def sum_waiting():
            if waiting["sum"] is None:
                return
            b, r, first, weighted, accs, summed, longer = waiting["sum"]
            waiting["sum"] = None
            for xc, acc in enumerate(accs):
                for j in range(CHUNK_GROUPS):
                    nc.tensor.matmul(
                        acc[:, j * P : (j + 1) * P],
                        lhsT=weighted[:, xc * BANK + j * P : xc * BANK + (j + 1) * P],
                        rhs=identity_f32[:],
                        is_transpose=True,
                        start=(r == 0 and j == 0),
                        stop=(r == ROUTES - 1 and j == CHUNK_GROUPS - 1),
                    )
                if r == ROUTES - 1:
                    turned = ring.tile([P, BANK], BF16, name="turned")
                    nc.scalar.copy(turned[:], acc[:])
                    back = psum.tile([P, BANK], BF16, name="bank", bufs=SHARED_BANKS)
                    for j in range(CHUNK_GROUPS):
                        nc.tensor.transpose(back[:, j * P : (j + 1) * P], turned[:, j * P : (j + 1) * P], identity[:])
                    nc.scalar.copy(att[b][:, first + xc * BANK : first + (xc + 1) * BANK], back[:])
            if r > 0 and longer is not None:
                nc.vector.tensor_tensor(longer, summed, weighted[:, len(accs) * BANK :], ALU.add)

        bias_of = {"key": None, "q": bias_q, "val": bias_v}
        table_bufs = {"key": 2, "q": 2, "val": 2}
        scores = psum.tile([P, BLOCKS, ROUTES, BLOCK_HEADS, GROUPS], F32, name="bank", bufs=SHARED_BANKS)

        def project_sums(name, b, first, count=BANK):
            xc, inside = divmod(first, BANK)
            acc = psum.tile([P, BANK], F32, name="bank", bufs=SHARED_BANKS)
            for kb in range(BLOCKS):
                nc.tensor.matmul(
                    acc[:, 0:count],
                    lhsT=weights_of[name, b][:, kb, :],
                    rhs=x_bf[xc][:, kb, inside : inside + count],
                    start=(kb == 0),
                    stop=(kb == BLOCKS - 1),
                )
            return acc

        def store_sums(name, b, first, acc, count=BANK):
            if first == 0:
                table[name, b] = tables.tile([P, TOKENS], F32, name=name, bufs=table_bufs[name])
            columns = table[name, b][:, first : first + count]
            if bias_of[name] is None:
                nc.scalar.copy(columns, acc[:, 0:count])
            else:
                nc.scalar.activation(columns, acc[:, 0:count], ACT.Identity, bias=bias_of[name][:, b : b + 1])

        def small_tile(name):
            return soft.tile([P, PAIR, HEAD_GROUPS], F32, name=name)

        def full_tile(name):
            return soft.tile([P, PAIR, ROUTES, HEAD_GROUPS], F32, name=name)

        def routes_last(columns):
            return columns.rearrange("p b r k -> p b k r")

        def over_routes(small):
            return small[:].unsqueeze(2).to_broadcast([P, PAIR, ROUTES, HEAD_GROUPS])

        def parked_rows(b):
            return out[b * BLOCK_ROWS : (b + 1) * BLOCK_ROWS, :]

        def rows_bank():
            return psum.tile([P, PAIR * P], F32, name="bank", bufs=SHARED_BANKS)

        def rows_tile(name):
            return soft.tile([P, PAIR * P], F32, name=name)

        def turn_to_rows(bank, columns, last):
            for j in range(PAIR):
                nc.tensor.matmul(
                    bank[:, j * P : (j + 1) * P],
                    lhsT=columns[:, j, :, :].rearrange("p r k -> p (r k)"),
                    rhs=identity_f32[:],
                    is_transpose=True,
                    start=(j == 0),
                    stop=(last and j == PAIR - 1),
                )

        def park(pair, p_rows):
            for j in range(PAIR):
                nc.sync.dma_start(
                    parked_rows(pair * PAIR + j).rearrange("q (g i) -> (q g) i", i=P), p_rows[:, j * P : (j + 1) * P]
                )

        def softmax_step(pair, step):
            pair_scores = scores[:, pair * PAIR : (pair + 1) * PAIR, :, :, :].rearrange("p b r h g -> p b r (h g)")
            if step == 0:
                top[pair] = small_tile("top")
                nc.vector.tensor_reduce(out=top[pair][:], in_=routes_last(pair_scores), axis=AXIS.X, op=ALU.max)
            elif step == 1:
                shifted = full_tile("shifted")
                nc.vector.tensor_tensor(shifted[:], pair_scores, over_routes(top[pair]), ALU.subtract)
                if pair == 0:
                    exps[pair] = full_tile("exps")
                    nc.scalar.activation(exps[pair][:], shifted[:], ACT.Exp, scale=SCALE)
                else:
                    shifted_rows = rows_bank()
                    turn_to_rows(shifted_rows, shifted, True)
                    exp_rows = rows_tile("exp_rows")
                    nc.scalar.activation(exp_rows[:], shifted_rows[:], ACT.Exp, scale=SCALE)
                    sum_rows = rows_bank()
                    nc.tensor.matmul(
                        sum_rows[:], lhsT=same_head_group[:].rearrange("p r k -> p (r k)"), rhs=exp_rows[:], start=True, stop=True
                    )
                    log_rows = rows_tile("log_rows")
                    nc.scalar.activation(log_rows[:], sum_rows[:], ACT.Ln)
                    exponent_rows = rows_bank()
                    turn_to_rows(exponent_rows, shifted, False)
                    nc.tensor.matmul(exponent_rows[:], lhsT=minus_inverse_scale[:], rhs=log_rows[:], start=False, stop=True)
                    p_rows = rows_tile("p_rows")
                    nc.scalar.activation(p_rows[:], exponent_rows[:], ACT.Exp, scale=SCALE)
                    park(pair, p_rows)
            elif step == 2 and pair == 0:
                total = small_tile("total")
                nc.vector.tensor_reduce(out=total[:], in_=routes_last(exps[pair][:]), axis=AXIS.X, op=ALU.add)
                inverse = small_tile("inverse")
                nc.vector.reciprocal(inverse[:], total[:])
                prob = full_tile("prob")
                nc.vector.tensor_tensor(prob[:], exps[pair][:], over_routes(inverse), ALU.mult)
                prob_rows = rows_bank()
                turn_to_rows(prob_rows, prob, True)
                p_rows = rows_tile("p_rows")
                nc.scalar.copy(p_rows[:], prob_rows[:])
                park(pair, p_rows)

        with tc.tile_pool(name="late", bufs=2) as late:

            def load_p(unit):
                if not 0 <= unit < BLOCKS * ROUTES:
                    return
                b, which = divmod(unit, ROUTES)
                p_of[unit] = late.tile([P, TOKENS], F32, name="p_block", bufs=P_AHEAD)
                by_head = parked_rows(b).rearrange("(r h) t -> h r t", h=BLOCK_HEADS)
                for h in range(BLOCK_HEADS):
                    channels = head_partitions(p_of[unit], h)
                    if b < LAST:
                        rows = by_head[h : h + 1, which, :]
                        nc.sync.dma_start(channels, rows.to_broadcast([HEAD_DIM, TOKENS]))
                    else:
                        rows = by_head[h : h + 1, :, which * BANK : (which + 1) * BANK]
                        nc.sync.dma_start(
                            channels.rearrange("c (r t) -> c r t", r=ROUTES), rows.to_broadcast([HEAD_DIM, ROUTES, BANK])
                        )

            def add_route(b, r, first, count, p_columns, accs, summed):
                if count == TOKENS:
                    weighted = ring.tile([P, count], F32, name="prod")
                else:
                    weighted = late.tile([P, count], F32, name="weighted_piece", bufs=2 * ROUTES)
                gather_times(weighted[:], table["val", b], r, first, count, p_columns)
                own = len(accs) * BANK
                if own == count:
                    longer = None
                elif r == 0:
                    longer = weighted[:, own:]
                elif r < ROUTES - 1:
                    longer = late.tile([P, count - own], F32, name="longer")[:]
                else:
                    longer = att[b][:, first + own : first + count]
                waiting["sum"] = (b, r, first, weighted, accs, summed, longer)
                return longer

            def out_terms(accs, kb, first, count):
                for ob in range(BLOCKS):
                    nc.tensor.matmul(
                        accs[ob][:, 0:count],
                        lhsT=w_out[:, kb, ob * P : (ob + 1) * P],
                        rhs=att[kb][:, first : first + count],
                        start=(kb == 0),
                        stop=(kb == LAST),
                    )

            def open_out(first, count):
                accs = [psum.tile([P, BANK], F32, name="bank", bufs=SHARED_BANKS) for ob in range(BLOCKS)]
                for kb in range(LAST):
                    out_terms(accs, kb, first, count)
                return accs

            def close_out(first, count, accs):
                out_terms(accs, LAST, first, count)
                for ob in range(BLOCKS):
                    result = late.tile([P, count], F32, name="result", bufs=2 * BLOCKS)
                    if first + count == TOKENS and ob % 2 == 1:
                        nc.vector.tensor_scalar_add(result[:], accs[ob][:, 0:count], bias_out[:, ob : ob + 1])
                    else:
                        nc.scalar.activation(result[:], accs[ob][:, 0:count], ACT.Identity, bias=bias_out[:, ob : ob + 1])
                    nc.sync.dma_start(out[ob * P : (ob + 1) * P, first : first + count], result[:])

            def sum_heads(b, r, prod):
                prod_bf = ring.tile([P, TOKENS], BF16, name="prod_bf")
                nc.scalar.copy(prod_bf[:], prod[:])
                for g in range(GROUPS):
                    nc.tensor.matmul(
                        scores[:, b, r, :, g], lhsT=prod_bf[:, g * P : (g + 1) * P], rhs=head_of[:], start=True, stop=True
                    )

            for xc in range(CHUNKS // 2):
                for name in ("key", "q"):
                    store_sums(name, 0, xc * BANK, project_sums(name, 0, xc * BANK))
            for first, count in CHUNKS_LAST_HALVED[CHUNKS // 2 :]:
                store_sums("key", 0, first, project_sums("key", 0, first, count), count)
            for xc in range(CHUNKS // 2, CHUNKS):
                store_sums("q", 0, xc * BANK, project_sums("q", 0, xc * BANK))

            ahead_of = [[("key", 1), ("q", 1)], [("key", 2), ("q", 2)], [("key", 3), ("q", 3)], [("val", 0)]]
            previous = None
            for b in range(BLOCKS):
                if b == LAST:
                    mix_val_weights(0)
                for r in range(ROUTES):
                    prod = ring.tile([P, TOKENS], F32, name="prod")
                    count = TOKENS // 2 if previous is None else TOKENS
                    for first in range(0, TOKENS, count):
                        tokens = slice(first, first + count)
                        gather_times(prod[:, tokens], table["key", b], r, first, count, table["q", b][:, tokens])
                    accs = [project_sums(name, block, r * BANK) for name, block in ahead_of[b]]
                    if previous is not None:
                        sum_heads(*previous)
                    for (name, block), acc in zip(ahead_of[b], accs):
                        store_sums(name, block, r * BANK, acc)
                    if b == PAIR:
                        softmax_step(0, r - 1)
                    if (b, r) == (LAST, 0):
                        for unit in range(P_AHEAD):
                            load_p(unit)
                    previous = (b, r, prod)
            sum_heads(*previous)

            for b in range(LAST):
                accs = [psum.tile([P, BANK], F32, name="bank", bufs=SHARED_BANKS) for xc in range(CHUNKS)]
                mix_val_weights(b + 1)
                for r in range(ROUTES):
                    unit = b * ROUTES + r
                    add_route(b, r, 0, TOKENS, p_of[unit][:], accs, None)
                    store_sums("val", b + 1, r * BANK, project_sums("val", b + 1, r * BANK))
                    softmax_step(1, unit)
                    load_p(unit + P_AHEAD)

            summed_piece = None
            for first, count in CHUNKS_LAST_HALVED:
                xc, inside = divmod(first, BANK)
                unit = LAST * ROUTES + xc
                accs = [psum.tile([P, BANK], F32, name="bank", bufs=SHARED_BANKS)] if xc < LAST_TENSOR_CHUNKS else []
                summed = None
                for r in range(ROUTES):
                    p_first = r * BANK + inside
                    summed = add_route(LAST, r, first, count, p_of[unit][:, p_first : p_first + count], accs, summed)
                    if r == 0:
                        if summed_piece is not None:
                            close_out(*summed_piece)
                        opened = open_out(first, count)
                summed_piece = (first, count, opened)
            sum_waiting()
            close_out(*summed_piece)
